import numpy as np
import ml_dtypes


def mxq(x, axis, fmt="e4m3"):
    dtype, down = {"e4m3": (ml_dtypes.float8_e4m3fn, 7), "e5m2": (ml_dtypes.float8_e5m2, 14)}[fmt]
    v = np.moveaxis(np.asarray(x, np.float32).astype(ml_dtypes.bfloat16).astype(np.float64), axis, -1)
    blocks = v.reshape(v.shape[:-1] + (-1, 32))
    amax = np.abs(blocks).max(-1, keepdims=True)
    byte = np.maximum(np.where(amax > 0, np.frexp(amax)[1] - 1 + 127, 0) - down, 1)
    scale = np.exp2(byte - 127.0)
    codes = (blocks / scale).astype(np.float32).astype(dtype).astype(np.float64)
    return np.moveaxis((codes * scale).reshape(v.shape), -1, axis)


WIDE = False


def mx_kscale(k):
    if not WIDE:
        return np.ones(k)
    levels = np.array([10, -10, 5, -5, 0])
    a = np.random.permutation(np.resize(levels, k // 512 * 4)).reshape(k // 512, 4)
    idx = np.arange(k)
    return np.exp2(a[idx // 512, idx % 128 // 32])


BF16 = ml_dtypes.bfloat16


def bf(x):
    return np.asarray(x, np.float32).astype(BF16)


def f64(x):
    return np.asarray(x).astype(np.float64)


B, I, H, P = 512, 1024, 1024, 1024
CLOCKS = (0.5, 0.8, 0.95, 0.999)
TWO_PI = 2.0 * np.pi


def sigmoid(v):
    return 1.0 / (1.0 + np.exp(-v))


def setup_inputs():
    s = mx_kscale(I)
    return {
        "x": bf(np.random.standard_normal((B, I)) * s),
        "h_state": bf(np.random.standard_normal((B, H))),
        "local_angle": bf(np.random.uniform(0.0, TWO_PI, (B, H))),
        "persistence": bf(np.repeat(np.asarray(CLOCKS), H // len(CLOCKS))),
        "weight_ih": bf(np.random.standard_normal((I, 3 * H)) * 0.7 / np.sqrt(I) / s[:, None]),
        "weight_hh": bf(np.random.standard_normal((H, 3 * H)) * 0.7 / np.sqrt(H)),
        "bias": bf(np.random.standard_normal(3 * H) * 0.3),
    }


def reference(x, h_state, local_angle, persistence, weight_ih, weight_hh, bias):
    h = f64(h_state)
    gates = ((mxq(f64(x), 1, "e4m3") @ mxq(f64(weight_ih), 0, "e4m3"))
             + (mxq(h, 1, "e4m3") @ mxq(f64(weight_hh), 0, "e4m3")) + f64(bias))
    r_gate, z_gate, n_gate = np.split(gates, 3, axis=-1)
    r = sigmoid(r_gate)
    z = sigmoid(z_gate)
    n = np.tanh(r * n_gate)
    phi_shift = z * TWO_PI
    raw_angle = f64(local_angle) * f64(persistence) + phi_shift
    h_blend = (1.0 - z) * h + z * n
    return (h_blend, raw_angle)

@@ -1,0 +1,329 @@
+import math
+from contextlib import ExitStack
+
+import concourse.mybir as mybir
+from concourse.masks import make_identity
+
+FLOPS = 2 * 512 * 2048 * 3072
+
+BF16 = mybir.dt.bfloat16
+F32 = mybir.dt.float32
+U32 = mybir.dt.uint32
+U8 = mybir.dt.uint8
+FP8X4 = mybir.dt.float8_e4m3fn_x4
+ACT = mybir.ActivationFunctionType
+ALU = mybir.AluOpType
+
+P = 128
+PIN = False
+AV = 512
+RAW_BUFS = 7
+TWO_PI = 2.0 * math.pi
+GATE_COL = (0, 2048, 1024)
+GATE_BIAS = (0, 16, 8)
+
+
+def tile_yarnixcellv4_pa_kernel(
+    tc, x, h_state, local_angle, persistence, weight_ih, weight_hh, bias, out_0, out_1
+):
+    nc = tc.nc
+    with ExitStack() as ctx:
+        if PIN:
+            ctx.enter_context(tc.manual_schedule())
+        const = ctx.enter_context(tc.tile_pool(name="const", bufs=1))
+        rawp = ctx.enter_context(tc.tile_pool(name="rawp", bufs=RAW_BUFS))
+        gwp = ctx.enter_context(tc.tile_pool(name="gwp", bufs=3))
+        wcp = ctx.enter_context(tc.tile_pool(name="wcp", bufs=2))
+        stp = ctx.enter_context(tc.tile_pool(name="stp", bufs=2))
+        mxp = ctx.enter_context(tc.psum_pool(name="mxp", bufs=4))
+        tpp = ctx.enter_context(tc.psum_pool(name="tpp", bufs=4))
+
+        ident_b = const.tile([P, P], BF16, name="ident_b")
+        ident_f = const.tile([P, P], F32, name="ident_f")
+        make_identity(nc, ident_f[:])
+        make_identity(nc, ident_b[:])
+        bp = const.tile([P, P], BF16, name="bp")
+        bcol = const.tile([P, 32], F32, name="bcol")
+        persp = const.tile([P, 8], F32, name="persp")
+        h_sb = const.tile([P, 4096], BF16, name="h_sb")
+        gh = const.tile([P, 4096], BF16, name="gh", align_bytes=64)
+        ang_t = const.tile([P, 8, 512], BF16, name="ang_t")
+        xc = const.tile([P, 1024], U32, name="xc", align_bytes=64)
+        xs = const.tile([P, 1024], U8, name="xs", align_bytes=64)
+        hc = const.tile([P, 1024], U32, name="hc", align_bytes=64)
+        hs = const.tile([P, 1024], U8, name="hs", align_bytes=64)
+        rt = const.tile([P, 8, 512], F32, name="rt")
+        zt = const.tile([P, 8, 512], F32, name="zt")
+
+        nc.vector.memset(bp[:], 0.0)
+        nc.scalar.dma_start(out=bp[0:24, :], in_=bias.rearrange("(r c) -> r c", c=P))
+        nc.scalar.dma_start(out=bp[24:32, :], in_=persistence.rearrange("(r c) -> r c", c=P))
+
+        raws = {}
+        wcs = {}
+        wss = {}
+        gws = {}
+
+        def load_w(i):
+            ph, c = divmod(i, 4)
+            col = GATE_COL[ph]
+            t = rawp.tile([P, 4, 1024], BF16, name="raw%d" % i, tag="raw")
+            if c < 2:
+                for u in range(2):
+                    r0 = 512 * c + 256 * u
+                    nc.sync.dma_start(
+                        out=t[:, 2 * u : 2 * u + 2, :],
+                        in_=weight_ih[r0 : r0 + 256, col : col + 1024].rearrange("(q e) w -> q e w", e=2),
+                    )
+            else:
+                r0 = 512 * (c - 2)
+                nc.sync.dma_start(
+                    out=t[:],
+                    in_=weight_hh[r0 : r0 + 512, col : col + 1024].rearrange("(t q) w -> q t w", q=P),
+                )
+            raws[i] = t
+
+        def load_rows(key, src):
+            t = rawp.tile([P, 4096], BF16, name="rows_%s" % key, tag="raw")
+            nc.sync.dma_start(
+                out=t[:].rearrange("p (b k) -> p b k", b=4),
+                in_=src.rearrange("(b p) k -> p b k", p=P),
+            )
+            raws[key] = t
+
+        load_seq = [0, "x", 1, 2, 3, 4, 5, 6, 7, "a", 8, 9, 10, 11]
+        load_pos = [0]
+
+        def next_load():
+            k = load_pos[0]
+            if k >= len(load_seq):
+                return
+            load_pos[0] = k + 1
+            key = load_seq[k]
+            if key == "x":
+                load_rows("x", x)
+            elif key == "a":
+                load_rows("a", local_angle)
+            else:
+                load_w(key)
+
+        def regroup(i):
+            raw = raws[i]
+            gw = gwp.tile([P, 1024, 4], BF16, name="gw%d" % i, tag="gw", align_bytes=64)
+            nc.vector.tensor_copy(
+                out=gw[:, 0:AV, :].rearrange("p (c i) t -> p c t i", i=4),
+                in_=raw[:, :, 0:AV].rearrange("p t (c i) -> p c t i", i=4),
+            )
+            nc.scalar.copy(
+                out=gw[:, AV:1024, :].rearrange("p (c i) t -> p c t i", i=4),
+                in_=raw[:, :, AV:1024].rearrange("p t (c i) -> p c t i", i=4),
+            )
+            gws[i] = gw
+            next_load()
+
+        def quant(i):
+            ph, c = divmod(i, 4)
+            if c == 0:
+                wcs[ph] = wcp.tile([P, 4, 1024], U32, name="wc%d" % ph, tag="wc", align_bytes=64)
+                wss[ph] = wcp.tile([P, 4, 1024], U8, name="ws%d" % ph, tag="ws", align_bytes=64)
+            nc.vector.quantize_mx(
+                out=wcs[ph][:, c, :].bitcast(FP8X4),
+                scales=wss[ph][:, c, :],
+                in_=gws[i][:].rearrange("p w t -> p (w t)"),
+            )
+
+        def x_front():
+            x_sb = raws["x"]
+            gx = gwp.tile([P, 4096], BF16, name="gx", tag="gw", align_bytes=64)
+            xw = x_sb[:].bitcast(F32)
+            gxw = gx[:].bitcast(F32)
+            for g in range(2):
+                for hf in range(2):
+                    xt = tpp.tile([P, 2, 256], F32, name="xt", tag="tp")
+                    for u in range(2):
+                        for b2 in range(2):
+                            w0 = (2 * hf + b2) * 512 + 256 * g + 128 * u
+                            nc.tensor.transpose(
+                                xt[:, u, 128 * b2 : 128 * b2 + 128], xw[:, w0 : w0 + 128], ident_f[:]
+                            )
+                    o0 = g * 1024 + hf * 512
+                    nc.scalar.copy(
+                        out=gxw[:, o0 : o0 + 512].rearrange("p (r u) -> p r u", u=2),
+                        in_=xt[:].rearrange("p u r -> p r u"),
+                    )
+            next_load()
+            return gx
+
+        def h_front():
+            for g in range(2):
+                for hf in range(2):
+                    ht = tpp.tile([P, 4, 256], BF16, name="ht", tag="tp")
+                    for t in range(4):
+                        for b2 in range(2):
+                            k0 = (2 * hf + b2) * 1024 + 512 * g + 128 * t
+                            nc.tensor.transpose(
+                                ht[:, t, 128 * b2 : 128 * b2 + 128], h_sb[:, k0 : k0 + 128], ident_b[:]
+                            )
+                    o0 = g * 2048 + hf * 1024
+                    nc.scalar.copy(
+                        out=gh[:, o0 : o0 + 1024].rearrange("p (r t) -> p r t", t=4),
+                        in_=ht[:].rearrange("p t r -> p r t"),
+                    )
+
+        def angle_front():
+            a_sb = raws["a"]
+            for jj in range(4):
+                at = tpp.tile([P, 2, 512], BF16, name="at", tag="tp")
+                for j2 in range(2):
+                    for b in range(4):
+                        k0 = b * 1024 + 128 * (2 * jj + j2)
+                        nc.tensor.transpose(
+                            at[:, j2, 128 * b : 128 * b + 128], a_sb[:, k0 : k0 + 128], ident_b[:]
+                        )
+                nc.scalar.copy(out=ang_t[:, 2 * jj : 2 * jj + 2, :], in_=at[:])
+            next_load()
+
+        accs = {}
+
+        def mx_pass(ph, j, c):
+            if c == 0:
+                accs[(ph, j)] = mxp.tile([P, 512], F32, name="acc%d_%d" % (ph, j), tag="acc")
+            acc = accs[(ph, j)]
+            if c < 2:
+                rc, rs, g = xc, xs, c
+            else:
+                rc, rs, g = hc, hs, c - 2
+            nc.tensor.matmul_mx(
+                out=acc[:],
+                lhsT=wcs[ph][:, c, 128 * j : 128 * j + 128].bitcast(FP8X4),
+                lhsT_scale=wss[ph][:, c, 128 * j : 128 * j + 128],
+                rhs=rc[:, 512 * g : 512 * g + 512].bitcast(FP8X4),
+                rhs_scale=rs[:, 512 * g : 512 * g + 512],
+                start=(c == 0),
+                stop=(c == 3),
+            )
+
+        def bias_col(ph, j):
+            k = GATE_BIAS[ph] + j
+            return bcol[:, k : k + 1]
+
+        def gate_out(ph, j):
+            acc = accs[(ph, j)]
+            if ph == 0:
+                nc.scalar.activation(out=rt[:, j, :], in_=acc[:], func=ACT.Sigmoid, bias=bias_col(ph, j), scale=1.0)
+            elif ph == 1:
+                nc.vector.scalar_tensor_tensor(
+                    out=rt[:, j, :], in0=acc[:], scalar=bias_col(ph, j), in1=rt[:, j, :], op0=ALU.add, op1=ALU.mult
+                )
+                nc.scalar.activation(out=rt[:, j, :], in_=rt[:, j, :], func=ACT.Tanh)
+            else:
+                nc.scalar.activation(out=zt[:, j, :], in_=acc[:], func=ACT.Sigmoid, bias=bias_col(ph, j), scale=1.0)
+
+        def n_minus_h(g):
+            nc.vector.tensor_tensor(
+                out=rt[:, 4 * g : 4 * g + 4, :],
+                in0=rt[:, 4 * g : 4 * g + 4, :],
+                in1=gh[:, 2048 * g : 2048 * g + 2048].rearrange("p (r t) -> p t r", t=4),
+                op=ALU.subtract,
+            )
+
+        for k in range(3):
+            next_load()
+        nc.sync.dma_start(
+            out=h_sb[:].rearrange("p (b k) -> p b k", b=4),
+            in_=h_state.rearrange("(b p) k -> p b k", p=P),
+        )
+        for k in range(RAW_BUFS - 3):
+            next_load()
+
+        pb = tpp.tile([P, P], BF16, name="pb", tag="tp")
+        nc.tensor.transpose(pb[:], bp[:], ident_b[:])
+        nc.vector.tensor_copy(out=bcol[:], in_=pb[:, 0:32])
+        nc.vector.tensor_scalar_mul(out=persp[:], in0=bcol[:, 24:32], scalar1=1.0 / TWO_PI)
+
+        SET0 = (0, 1, 2, 3)
+        SET1 = (4, 5, 6, 7)
+
+        regroup(0)
+        gx = x_front()
+        regroup(1)
+        nc.vector.quantize_mx(out=xc[:].bitcast(FP8X4), scales=xs[:], in_=gx[:])
+        quant(0)
+        for j in SET0:
+            mx_pass(0, j, 0)
+        h_front()
+        regroup(2)
+        quant(1)
+        for j in SET0:
+            mx_pass(0, j, 1)
+        nc.vector.quantize_mx(out=hc[:].bitcast(FP8X4), scales=hs[:], in_=gh[:])
+        regroup(3)
+        quant(2)
+        for j in SET0:
+            mx_pass(0, j, 2)
+
+        for ph in range(3):
+            if ph < 2:
+                regroup(4 * ph + 4)
+            quant(4 * ph + 3)
+            for j in SET0:
+                mx_pass(ph, j, 3)
+            if ph < 2:
+                for j in SET0:
+                    gate_out(ph, j)
+                for j in SET1:
+                    for c in range(4):
+                        mx_pass(ph, j, c)
+                    gate_out(ph, j)
+                for c in range(3):
+                    if ph == 1 and c == 0:
+                        angle_front()
+                    regroup(4 * ph + 5 + c)
+                    quant(4 * ph + 4 + c)
+                    for j in SET0:
+                        mx_pass(ph + 1, j, c)
+                    if ph == 1 and c < 2:
+                        n_minus_h(c)
+
+        for j in SET0:
+            gate_out(2, j)
+        h_nat = h_sb[:].rearrange("p (b k) -> p b k", b=4)
+        out0_v = out_0.rearrange("(b p) u -> p b u", p=P)
+        out1_v = out_1.rearrange("(b p) u -> p b u", p=P)
+        banks = {}
+        stages = {}
+        for j in range(9):
+            if j < 8:
+                if j + 4 < 8:
+                    for c in range(4):
+                        mx_pass(2, j + 4, c)
+                    gate_out(2, j + 4)
+                nc.vector.tensor_tensor(out=rt[:, j, :], in0=rt[:, j, :], in1=zt[:, j, :], op=ALU.mult)
+                nc.vector.scalar_tensor_tensor(
+                    out=zt[:, j, :], in0=ang_t[:, j, :], scalar=persp[:, j : j + 1], in1=zt[:, j, :],
+                    op0=ALU.mult, op1=ALU.add,
+                )
+                pe = tpp.tile([P, 4, P], F32, name="pe", tag="tp")
+                pq = tpp.tile([P, 4, P], F32, name="pq", tag="tp")
+                for b in range(4):
+                    nc.tensor.transpose(pe[:, b, :], rt[:, j, 128 * b : 128 * b + 128], ident_f[:])
+                for b in range(4):
+                    nc.tensor.transpose(pq[:, b, :], zt[:, j, 128 * b : 128 * b + 128], ident_f[:])
+                banks[j] = (pe, pq)
+            if j >= 1:
+                i = j - 1
+                pe, pq = banks[i]
+                if i % 2 == 0:
+                    hb_st = stp.tile([P, 4, 256], F32, name="hb_st", tag="hb")
+                    ra_st = stp.tile([P, 4, 256], F32, name="ra_st", tag="ra")
+                    stages[i // 2] = (hb_st, ra_st)
+                hb_st, ra_st = stages[i // 2]
+                o = 128 * (i % 2)
+                nc.vector.tensor_tensor(
+                    out=hb_st[:, :, o : o + 128], in0=pe[:], in1=h_nat[:, :, 128 * i : 128 * i + 128], op=ALU.add
+                )
+                nc.scalar.activation(out=ra_st[:, :, o : o + 128], in_=pq[:], func=ACT.Copy, scale=TWO_PI)
+                if i % 2 == 1:
+                    u0 = 256 * (i // 2)
+                    nc.sync.dma_start(out=out0_v[:, :, u0 : u0 + 256], in_=hb_st[:])
+                    nc.sync.dma_start(out=out1_v[:, :, u0 : u0 + 256], in_=ra_st[:])

@@ -15,12 +15,13 @@ ACT = mybir.ActivationFunctionType
 ALU = mybir.AluOpType
 
 P = 128
-PIN = False
-AV = 512
+PIN = True
+AVS = (512, 768, 896)
 RAW_BUFS = 7
+QUANT_FIRST = 4
 TWO_PI = 2.0 * math.pi
-GATE_COL = (0, 2048, 1024)
-GATE_BIAS = (0, 16, 8)
+GATE_COL = (1024, 0, 2048)
+GATE_BIAS = (8, 0, 16)
 
 
 def tile_yarnixcellv4_pa_kernel(
@@ -34,6 +35,7 @@ def tile_yarnixcellv4_pa_kernel(
         rawp = ctx.enter_context(tc.tile_pool(name="rawp", bufs=RAW_BUFS))
         gwp = ctx.enter_context(tc.tile_pool(name="gwp", bufs=3))
         wcp = ctx.enter_context(tc.tile_pool(name="wcp", bufs=2))
+        app = ctx.enter_context(tc.tile_pool(name="app", bufs=3))
         stp = ctx.enter_context(tc.tile_pool(name="stp", bufs=2))
         mxp = ctx.enter_context(tc.psum_pool(name="mxp", bufs=4))
         tpp = ctx.enter_context(tc.psum_pool(name="tpp", bufs=4))
@@ -45,15 +47,15 @@ def tile_yarnixcellv4_pa_kernel(
         bp = const.tile([P, P], BF16, name="bp")
         bcol = const.tile([P, 32], F32, name="bcol")
         persp = const.tile([P, 8], F32, name="persp")
-        h_sb = const.tile([P, 4096], BF16, name="h_sb")
+        a_sb = const.tile([P, 4096], BF16, name="a_sb")
         gh = const.tile([P, 4096], BF16, name="gh", align_bytes=64)
-        ang_t = const.tile([P, 8, 512], BF16, name="ang_t")
         xc = const.tile([P, 1024], U32, name="xc", align_bytes=64)
         xs = const.tile([P, 1024], U8, name="xs", align_bytes=64)
         hc = const.tile([P, 1024], U32, name="hc", align_bytes=64)
         hs = const.tile([P, 1024], U8, name="hs", align_bytes=64)
-        rt = const.tile([P, 8, 512], F32, name="rt")
         zt = const.tile([P, 8, 512], F32, name="zt")
+        wt = const.tile([P, 8, 512], F32, name="wt")
+        rt = const.tile([P, 8, 512], F32, name="rt")
 
         nc.vector.memset(bp[:], 0.0)
         nc.scalar.dma_start(out=bp[0:24, :], in_=bias.rearrange("(r c) -> r c", c=P))
@@ -83,15 +85,13 @@ def tile_yarnixcellv4_pa_kernel(
                 )
             raws[i] = t
 
-        def load_rows(key, src):
-            t = rawp.tile([P, 4096], BF16, name="rows_%s" % key, tag="raw")
+        def load_rows(t, src):
             nc.sync.dma_start(
                 out=t[:].rearrange("p (b k) -> p b k", b=4),
-                in_=src.rearrange("(b p) k -> p b k", p=P),
+                in_=src.rearrange("(p b) k -> p b k", b=4),
             )
-            raws[key] = t
 
-        load_seq = [0, "x", 1, 2, 3, 4, 5, 6, 7, "a", 8, 9, 10, 11]
+        load_seq = ["x", "h", 0, 1, 2, 3, 4, "a", 5, 6, 7, 8, 9, 10, 11]
         load_pos = [0]
 
         def next_load():
@@ -100,23 +100,33 @@ def tile_yarnixcellv4_pa_kernel(
                 return
             load_pos[0] = k + 1
             key = load_seq[k]
-            if key == "x":
-                load_rows("x", x)
-            elif key == "a":
-                load_rows("a", local_angle)
+            if key == "a":
+                load_rows(a_sb, local_angle)
+                next_load()
+            elif key == "x" or key == "h":
+                t = rawp.tile([P, 4096], BF16, name="rows_%s" % key, tag="raw")
+                load_rows(t, x if key == "x" else h_state)
+                raws[key] = t
             else:
                 load_w(key)
 
+        def copy_on(k, out, in_):
+            if k % 2 == 0:
+                nc.scalar.copy(out=out, in_=in_)
+            else:
+                nc.vector.tensor_copy(out=out, in_=in_)
+
         def regroup(i):
             raw = raws[i]
+            av = AVS[i // 4]
             gw = gwp.tile([P, 1024, 4], BF16, name="gw%d" % i, tag="gw", align_bytes=64)
             nc.vector.tensor_copy(
-                out=gw[:, 0:AV, :].rearrange("p (c i) t -> p c t i", i=4),
-                in_=raw[:, :, 0:AV].rearrange("p t (c i) -> p c t i", i=4),
+                out=gw[:, 0:av, :].rearrange("p (c i) t -> p c t i", i=4),
+                in_=raw[:, :, 0:av].rearrange("p t (c i) -> p c t i", i=4),
             )
             nc.scalar.copy(
-                out=gw[:, AV:1024, :].rearrange("p (c i) t -> p c t i", i=4),
-                in_=raw[:, :, AV:1024].rearrange("p t (c i) -> p c t i", i=4),
+                out=gw[:, av:1024, :].rearrange("p (c i) t -> p c t i", i=4),
+                in_=raw[:, :, av:1024].rearrange("p t (c i) -> p c t i", i=4),
             )
             gws[i] = gw
             next_load()
@@ -131,57 +141,6 @@ def tile_yarnixcellv4_pa_kernel(
                 scales=wss[ph][:, c, :],
                 in_=gws[i][:].rearrange("p w t -> p (w t)"),
             )
-
-        def x_front():
-            x_sb = raws["x"]
-            gx = gwp.tile([P, 4096], BF16, name="gx", tag="gw", align_bytes=64)
-            xw = x_sb[:].bitcast(F32)
-            gxw = gx[:].bitcast(F32)
-            for g in range(2):
-                for hf in range(2):
-                    xt = tpp.tile([P, 2, 256], F32, name="xt", tag="tp")
-                    for u in range(2):
-                        for b2 in range(2):
-                            w0 = (2 * hf + b2) * 512 + 256 * g + 128 * u
-                            nc.tensor.transpose(
-                                xt[:, u, 128 * b2 : 128 * b2 + 128], xw[:, w0 : w0 + 128], ident_f[:]
-                            )
-                    o0 = g * 1024 + hf * 512
-                    nc.scalar.copy(
-                        out=gxw[:, o0 : o0 + 512].rearrange("p (r u) -> p r u", u=2),
-                        in_=xt[:].rearrange("p u r -> p r u"),
-                    )
-            next_load()
-            return gx
-
-        def h_front():
-            for g in range(2):
-                for hf in range(2):
-                    ht = tpp.tile([P, 4, 256], BF16, name="ht", tag="tp")
-                    for t in range(4):
-                        for b2 in range(2):
-                            k0 = (2 * hf + b2) * 1024 + 512 * g + 128 * t
-                            nc.tensor.transpose(
-                                ht[:, t, 128 * b2 : 128 * b2 + 128], h_sb[:, k0 : k0 + 128], ident_b[:]
-                            )
-                    o0 = g * 2048 + hf * 1024
-                    nc.scalar.copy(
-                        out=gh[:, o0 : o0 + 1024].rearrange("p (r t) -> p r t", t=4),
-                        in_=ht[:].rearrange("p t r -> p r t"),
-                    )
-
-        def angle_front():
-            a_sb = raws["a"]
-            for jj in range(4):
-                at = tpp.tile([P, 2, 512], BF16, name="at", tag="tp")
-                for j2 in range(2):
-                    for b in range(4):
-                        k0 = b * 1024 + 128 * (2 * jj + j2)
-                        nc.tensor.transpose(
-                            at[:, j2, 128 * b : 128 * b + 128], a_sb[:, k0 : k0 + 128], ident_b[:]
-                        )
-                nc.scalar.copy(out=ang_t[:, 2 * jj : 2 * jj + 2, :], in_=at[:])
-            next_load()
 
         accs = {}
 
@@ -203,127 +162,156 @@ def tile_yarnixcellv4_pa_kernel(
                 stop=(c == 3),
             )
 
+        def pair_tiles(q):
+            return (2 * (q % 4), 2 * (q % 4) + 1)
+
+        def first_slot(q, c):
+            return max(0 if q < 2 else q + 1, 4 * (q // 4) + c)
+
+        def passes(s, fresh):
+            for q in range(12):
+                if (q >= 2 and q == s - 1) != fresh:
+                    continue
+                for c in range(4):
+                    if first_slot(q, c) == s:
+                        for j in pair_tiles(q):
+                            mx_pass(q // 4, j, c)
+
         def bias_col(ph, j):
             k = GATE_BIAS[ph] + j
             return bcol[:, k : k + 1]
 
-        def gate_out(ph, j):
-            acc = accs[(ph, j)]
-            if ph == 0:
-                nc.scalar.activation(out=rt[:, j, :], in_=acc[:], func=ACT.Sigmoid, bias=bias_col(ph, j), scale=1.0)
-            elif ph == 1:
-                nc.vector.scalar_tensor_tensor(
-                    out=rt[:, j, :], in0=acc[:], scalar=bias_col(ph, j), in1=rt[:, j, :], op0=ALU.add, op1=ALU.mult
+        def h_t(j):
+            g, t = divmod(j, 4)
+            return gh[:, 2048 * g : 2048 * g + 2048].rearrange("p (r t) -> p t r", t=4)[:, t, :]
+
+        def add_transposed(bank, first, second):
+            for b in range(4):
+                cols = slice(128 * b, 128 * b + 128)
+                nc.tensor.matmul(
+                    out=bank[:, b, :], lhsT=first[:, cols], rhs=ident_f[:], is_transpose=True, start=True, stop=False
                 )
-                nc.scalar.activation(out=rt[:, j, :], in_=rt[:, j, :], func=ACT.Tanh)
-            else:
-                nc.scalar.activation(out=zt[:, j, :], in_=acc[:], func=ACT.Sigmoid, bias=bias_col(ph, j), scale=1.0)
+                nc.tensor.matmul(
+                    out=bank[:, b, :], lhsT=second[:, cols], rhs=ident_f[:], is_transpose=True, start=False, stop=True
+                )
 
-        def n_minus_h(g):
-            nc.vector.tensor_tensor(
-                out=rt[:, 4 * g : 4 * g + 4, :],
-                in0=rt[:, 4 * g : 4 * g + 4, :],
-                in1=gh[:, 2048 * g : 2048 * g + 2048].rearrange("p (r t) -> p t r", t=4),
-                op=ALU.subtract,
+        out0_v = out_0.rearrange("(p b) u -> p b u", b=4)
+        out1_v = out_1.rearrange("(p b) u -> p b u", b=4)
+        banks = {}
+        stages = {}
+
+        def leave(kind, j, scale, out_v):
+            if j % 2 == 0:
+                stages[kind] = stp.tile([P, 4, 256], F32, name="st_%s" % kind, tag=kind)
+            st = stages[kind]
+            o = 128 * (j % 2)
+            nc.scalar.activation(out=st[:, :, o : o + 128], in_=banks[(kind, j)][:], func=ACT.Copy, scale=scale)
+            if j % 2 == 1:
+                u0 = 128 * (j - 1)
+                nc.sync.dma_start(out=out_v[:, :, u0 : u0 + 256], in_=st[:])
+
+        for k in range(RAW_BUFS):
+            next_load()
+
+        gx = gwp.tile([P, 4096], BF16, name="gx", tag="gw", align_bytes=64)
+        xw = raws["x"][:].bitcast(F32)
+        gxw = gx[:].bitcast(F32)
+        for g in range(2):
+            for hf in range(2):
+                xt = tpp.tile([P, 2, 256], F32, name="xt", tag="tp")
+                for u in range(2):
+                    for b2 in range(2):
+                        w0 = (2 * hf + b2) * 512 + 256 * g + 128 * u
+                        nc.tensor.transpose(xt[:, u, 128 * b2 : 128 * b2 + 128], xw[:, w0 : w0 + 128], ident_f[:])
+                o0 = g * 1024 + hf * 512
+                copy_on(
+                    hf,
+                    gxw[:, o0 : o0 + 512].rearrange("p (r u) -> p r u", u=2),
+                    xt[:].rearrange("p u r -> p r u"),
+                )
+        next_load()
+        h_sb = raws["h"]
+        hts = []
+        for g in range(2):
+            for hf in range(2):
+                ht = tpp.tile([P, 4, 256], BF16, name="ht", tag="tp")
+                for t in range(4):
+                    for b2 in range(2):
+                        k0 = (2 * hf + b2) * 1024 + 512 * g + 128 * t
+                        nc.tensor.transpose(ht[:, t, 128 * b2 : 128 * b2 + 128], h_sb[:, k0 : k0 + 128], ident_b[:])
+                hts.append(ht)
+        nc.vector.quantize_mx(out=xc[:].bitcast(FP8X4), scales=xs[:], in_=gx[:])
+        for k in range(4):
+            copy_on(
+                k,
+                gh[:, 1024 * k : 1024 * k + 1024].rearrange("p (r t) -> p r t", t=4),
+                hts[k][:].rearrange("p t r -> p r t"),
             )
-
-        for k in range(3):
-            next_load()
-        nc.sync.dma_start(
-            out=h_sb[:].rearrange("p (b k) -> p b k", b=4),
-            in_=h_state.rearrange("(b p) k -> p b k", p=P),
-        )
-        for k in range(RAW_BUFS - 3):
-            next_load()
-
+        next_load()
+        nc.vector.quantize_mx(out=hc[:].bitcast(FP8X4), scales=hs[:], in_=gh[:])
         pb = tpp.tile([P, P], BF16, name="pb", tag="tp")
         nc.tensor.transpose(pb[:], bp[:], ident_b[:])
         nc.vector.tensor_copy(out=bcol[:], in_=pb[:, 0:32])
         nc.vector.tensor_scalar_mul(out=persp[:], in0=bcol[:, 24:32], scalar1=1.0 / TWO_PI)
 
-        SET0 = (0, 1, 2, 3)
-        SET1 = (4, 5, 6, 7)
-
         regroup(0)
-        gx = x_front()
-        regroup(1)
-        nc.vector.quantize_mx(out=xc[:].bitcast(FP8X4), scales=xs[:], in_=gx[:])
-        quant(0)
-        for j in SET0:
-            mx_pass(0, j, 0)
-        h_front()
-        regroup(2)
-        quant(1)
-        for j in SET0:
-            mx_pass(0, j, 1)
-        nc.vector.quantize_mx(out=hc[:].bitcast(FP8X4), scales=hs[:], in_=gh[:])
-        regroup(3)
-        quant(2)
-        for j in SET0:
-            mx_pass(0, j, 2)
-
-        for ph in range(3):
-            if ph < 2:
-                regroup(4 * ph + 4)
-            quant(4 * ph + 3)
-            for j in SET0:
-                mx_pass(ph, j, 3)
-            if ph < 2:
-                for j in SET0:
-                    gate_out(ph, j)
-                for j in SET1:
-                    for c in range(4):
-                        mx_pass(ph, j, c)
-                    gate_out(ph, j)
-                for c in range(3):
-                    if ph == 1 and c == 0:
-                        angle_front()
-                    regroup(4 * ph + 5 + c)
-                    quant(4 * ph + 4 + c)
-                    for j in SET0:
-                        mx_pass(ph + 1, j, c)
-                    if ph == 1 and c < 2:
-                        n_minus_h(c)
-
-        for j in SET0:
-            gate_out(2, j)
-        h_nat = h_sb[:].rearrange("p (b k) -> p b k", b=4)
-        out0_v = out_0.rearrange("(b p) u -> p b u", p=P)
-        out1_v = out_1.rearrange("(b p) u -> p b u", p=P)
-        banks = {}
-        stages = {}
-        for j in range(9):
-            if j < 8:
-                if j + 4 < 8:
-                    for c in range(4):
-                        mx_pass(2, j + 4, c)
-                    gate_out(2, j + 4)
-                nc.vector.tensor_tensor(out=rt[:, j, :], in0=rt[:, j, :], in1=zt[:, j, :], op=ALU.mult)
-                nc.vector.scalar_tensor_tensor(
-                    out=zt[:, j, :], in0=ang_t[:, j, :], scalar=persp[:, j : j + 1], in1=zt[:, j, :],
-                    op0=ALU.mult, op1=ALU.add,
-                )
-                pe = tpp.tile([P, 4, P], F32, name="pe", tag="tp")
-                pq = tpp.tile([P, 4, P], F32, name="pq", tag="tp")
-                for b in range(4):
-                    nc.tensor.transpose(pe[:, b, :], rt[:, j, 128 * b : 128 * b + 128], ident_f[:])
-                for b in range(4):
-                    nc.tensor.transpose(pq[:, b, :], zt[:, j, 128 * b : 128 * b + 128], ident_f[:])
-                banks[j] = (pe, pq)
-            if j >= 1:
-                i = j - 1
-                pe, pq = banks[i]
-                if i % 2 == 0:
-                    hb_st = stp.tile([P, 4, 256], F32, name="hb_st", tag="hb")
-                    ra_st = stp.tile([P, 4, 256], F32, name="ra_st", tag="ra")
-                    stages[i // 2] = (hb_st, ra_st)
-                hb_st, ra_st = stages[i // 2]
-                o = 128 * (i % 2)
-                nc.vector.tensor_tensor(
-                    out=hb_st[:, :, o : o + 128], in0=pe[:], in1=h_nat[:, :, 128 * i : 128 * i + 128], op=ALU.add
-                )
-                nc.scalar.activation(out=ra_st[:, :, o : o + 128], in_=pq[:], func=ACT.Copy, scale=TWO_PI)
-                if i % 2 == 1:
-                    u0 = 256 * (i // 2)
-                    nc.sync.dma_start(out=out0_v[:, :, u0 : u0 + 256], in_=hb_st[:])
-                    nc.sync.dma_start(out=out1_v[:, :, u0 : u0 + 256], in_=ra_st[:])
+        for s in range(17):
+            if s < QUANT_FIRST and s <= 11:
+                quant(s)
+            if s + 1 <= 11:
+                regroup(s + 1)
+            if s >= QUANT_FIRST and s <= 11:
+                quant(s)
+            passes(s, False)
+            q2 = s - 5
+            if 0 <= q2 < 4:
+                for j in pair_tiles(q2):
+                    leave("ra", j, TWO_PI, out1_v)
+            q3 = s - 5
+            if 8 <= q3 < 12:
+                for j in pair_tiles(q3):
+                    leave("hb", j, -1.0, out0_v)
+            q1 = s - 4
+            if 0 <= q1 < 4:
+                for j in pair_tiles(q1):
+                    nc.vector.scalar_tensor_tensor(
+                        out=wt[:, j, :], in0=zt[:, j, :], scalar=1.0, in1=h_t(j), op0=ALU.subtract, op1=ALU.mult
+                    )
+            if 8 <= q1 < 12:
+                for j in pair_tiles(q1):
+                    nc.vector.scalar_tensor_tensor(
+                        out=rt[:, j, :], in0=rt[:, j, :], scalar=-1.0, in1=zt[:, j, :], op0=ALU.mult, op1=ALU.mult
+                    )
+                    bank = tpp.tile([P, 4, P], F32, name="phb", tag="tp")
+                    add_transposed(bank, rt[:, j, :], wt[:, j, :])
+                    banks[("hb", j)] = bank
+            q = s - 3
+            if 0 <= q < 4:
+                at = tpp.tile([P, 2, 512], BF16, name="at", tag="tp")
+                for j2 in range(2):
+                    for b in range(4):
+                        k0 = b * 1024 + 128 * (2 * q + j2)
+                        nc.tensor.transpose(at[:, j2, 128 * b : 128 * b + 128], a_sb[:, k0 : k0 + 128], ident_b[:])
+                for j in pair_tiles(q):
+                    nc.scalar.activation(
+                        out=zt[:, j, :], in_=accs[(0, j)][:], func=ACT.Sigmoid, bias=bias_col(0, j), scale=1.0
+                    )
+                for j in pair_tiles(q):
+                    ap = app.tile([P, 512], F32, name="ap", tag="ap")
+                    nc.scalar.activation(out=ap[:], in_=at[:, j % 2, :], func=ACT.Copy, scale=persp[:, j : j + 1])
+                    bank = tpp.tile([P, 4, P], F32, name="pra", tag="tp")
+                    add_transposed(bank, zt[:, j, :], ap[:])
+                    banks[("ra", j)] = bank
+            elif 4 <= q < 8:
+                for j in pair_tiles(q):
+                    nc.scalar.activation(
+                        out=rt[:, j, :], in_=accs[(1, j)][:], func=ACT.Sigmoid, bias=bias_col(1, j), scale=1.0
+                    )
+            elif 8 <= q < 12:
+                for j in pair_tiles(q):
+                    nc.vector.scalar_tensor_tensor(
+                        out=rt[:, j, :], in0=accs[(2, j)][:], scalar=bias_col(2, j), in1=rt[:, j, :],
+                        op0=ALU.add, op1=ALU.mult,
+                    )
+                    nc.scalar.activation(out=rt[:, j, :], in_=rt[:, j, :], func=ACT.Tanh)
+            passes(s, True)

@@ -15,7 +15,7 @@ ACT = mybir.ActivationFunctionType
 ALU = mybir.AluOpType
 
 P = 128
-PIN = True
+PIN = False
 AVS = (512, 768, 896)
 RAW_BUFS = 7
 QUANT_FIRST = 4
@@ -36,7 +36,7 @@ def tile_yarnixcellv4_pa_kernel(
         gwp = ctx.enter_context(tc.tile_pool(name="gwp", bufs=3))
         wcp = ctx.enter_context(tc.tile_pool(name="wcp", bufs=2))
         app = ctx.enter_context(tc.tile_pool(name="app", bufs=3))
-        stp = ctx.enter_context(tc.tile_pool(name="stp", bufs=2))
+        stp = ctx.enter_context(tc.tile_pool(name="stp", bufs=3))
         mxp = ctx.enter_context(tc.psum_pool(name="mxp", bufs=4))
         tpp = ctx.enter_context(tc.psum_pool(name="tpp", bufs=4))
 

@@ -16,12 +16,12 @@ ALU = mybir.AluOpType
 
 P = 128
 PIN = False
-AVS = (512, 768, 896)
-RAW_BUFS = 7
-QUANT_FIRST = 4
+RAW_BUFS = 12
 TWO_PI = 2.0 * math.pi
 GATE_COL = (1024, 0, 2048)
 GATE_BIAS = (8, 0, 16)
+AV_FIRST = 320
+AVS = (192, 320, 384)
 
 
 def tile_yarnixcellv4_pa_kernel(
@@ -33,9 +33,9 @@ def tile_yarnixcellv4_pa_kernel(
             ctx.enter_context(tc.manual_schedule())
         const = ctx.enter_context(tc.tile_pool(name="const", bufs=1))
         rawp = ctx.enter_context(tc.tile_pool(name="rawp", bufs=RAW_BUFS))
-        gwp = ctx.enter_context(tc.tile_pool(name="gwp", bufs=3))
-        wcp = ctx.enter_context(tc.tile_pool(name="wcp", bufs=2))
-        app = ctx.enter_context(tc.tile_pool(name="app", bufs=3))
+        gwp = ctx.enter_context(tc.tile_pool(name="gwp", bufs=4))
+        wcp = ctx.enter_context(tc.tile_pool(name="wcp", bufs=3))
+        app = ctx.enter_context(tc.tile_pool(name="app", bufs=4))
         stp = ctx.enter_context(tc.tile_pool(name="stp", bufs=3))
         mxp = ctx.enter_context(tc.psum_pool(name="mxp", bufs=4))
         tpp = ctx.enter_context(tc.psum_pool(name="tpp", bufs=4))
@@ -47,7 +47,10 @@ def tile_yarnixcellv4_pa_kernel(
         bp = const.tile([P, P], BF16, name="bp")
         bcol = const.tile([P, 32], F32, name="bcol")
         persp = const.tile([P, 8], F32, name="persp")
+        x_sb = const.tile([P, 4096], BF16, name="x_sb")
+        h_sb = const.tile([P, 4096], BF16, name="h_sb")
         a_sb = const.tile([P, 4096], BF16, name="a_sb")
+        gx = const.tile([P, 4096], BF16, name="gx", align_bytes=64)
         gh = const.tile([P, 4096], BF16, name="gh", align_bytes=64)
         xc = const.tile([P, 1024], U32, name="xc", align_bytes=64)
         xs = const.tile([P, 1024], U8, name="xs", align_bytes=64)
@@ -66,49 +69,42 @@ def tile_yarnixcellv4_pa_kernel(
         wss = {}
         gws = {}
 
-        def load_w(i):
-            ph, c = divmod(i, 4)
-            col = GATE_COL[ph]
-            t = rawp.tile([P, 4, 1024], BF16, name="raw%d" % i, tag="raw")
+        def load_piece(i):
+            hg, c = divmod(i, 4)
+            col = GATE_COL[hg % 3] + 512 * (hg // 3)
+            t = rawp.tile([P, 4, 512], BF16, name="raw%d" % i, tag="raw")
             if c < 2:
                 for u in range(2):
                     r0 = 512 * c + 256 * u
                     nc.sync.dma_start(
                         out=t[:, 2 * u : 2 * u + 2, :],
-                        in_=weight_ih[r0 : r0 + 256, col : col + 1024].rearrange("(q e) w -> q e w", e=2),
+                        in_=weight_ih[r0 : r0 + 256, col : col + 512].rearrange("(q e) w -> q e w", e=2),
                     )
             else:
                 r0 = 512 * (c - 2)
                 nc.sync.dma_start(
                     out=t[:],
-                    in_=weight_hh[r0 : r0 + 512, col : col + 1024].rearrange("(t q) w -> q t w", q=P),
+                    in_=weight_hh[r0 : r0 + 512, col : col + 512].rearrange("(t q) w -> q t w", q=P),
                 )
             raws[i] = t
 
-        def load_rows(t, src):
-            nc.sync.dma_start(
-                out=t[:].rearrange("p (b k) -> p b k", b=4),
-                in_=src.rearrange("(p b) k -> p b k", b=4),
-            )
+        def load_rows(t, src, pieces):
+            tv = t[:].rearrange("p (b k) -> p b k", b=4)
+            sv = src.rearrange("(p b) k -> p b k", b=4)
+            n = 4 // pieces
+            for k in range(pieces):
+                nc.sync.dma_start(out=tv[:, n * k : n * k + n, :], in_=sv[:, n * k : n * k + n, :])
 
-        load_seq = ["x", "h", 0, 1, 2, 3, 4, "a", 5, 6, 7, 8, 9, 10, 11]
         load_pos = [0]
 
         def next_load():
             k = load_pos[0]
-            if k >= len(load_seq):
+            if k >= 24:
                 return
             load_pos[0] = k + 1
-            key = load_seq[k]
-            if key == "a":
-                load_rows(a_sb, local_angle)
-                next_load()
-            elif key == "x" or key == "h":
-                t = rawp.tile([P, 4096], BF16, name="rows_%s" % key, tag="raw")
-                load_rows(t, x if key == "x" else h_state)
-                raws[key] = t
-            else:
-                load_w(key)
+            load_piece(k)
+            if k == 3:
+                load_rows(a_sb, local_angle, 1)
 
         def copy_on(k, out, in_):
             if k % 2 == 0:
@@ -118,67 +114,52 @@ def tile_yarnixcellv4_pa_kernel(
 
         def regroup(i):
             raw = raws[i]
-            av = AVS[i // 4]
-            gw = gwp.tile([P, 1024, 4], BF16, name="gw%d" % i, tag="gw", align_bytes=64)
+            av = AV_FIRST if i < 4 else AVS[(i // 4) % 3]
+            gw = gwp.tile([P, 512, 4], BF16, name="gw%d" % i, tag="gw", align_bytes=64)
             nc.vector.tensor_copy(
                 out=gw[:, 0:av, :].rearrange("p (c i) t -> p c t i", i=4),
                 in_=raw[:, :, 0:av].rearrange("p t (c i) -> p c t i", i=4),
             )
             nc.scalar.copy(
-                out=gw[:, av:1024, :].rearrange("p (c i) t -> p c t i", i=4),
-                in_=raw[:, :, av:1024].rearrange("p t (c i) -> p c t i", i=4),
+                out=gw[:, av:512, :].rearrange("p (c i) t -> p c t i", i=4),
+                in_=raw[:, :, av:512].rearrange("p t (c i) -> p c t i", i=4),
             )
             gws[i] = gw
             next_load()
 
         def quant(i):
-            ph, c = divmod(i, 4)
+            hg, c = divmod(i, 4)
             if c == 0:
-                wcs[ph] = wcp.tile([P, 4, 1024], U32, name="wc%d" % ph, tag="wc", align_bytes=64)
-                wss[ph] = wcp.tile([P, 4, 1024], U8, name="ws%d" % ph, tag="ws", align_bytes=64)
+                wcs[hg] = wcp.tile([P, 4, 512], U32, name="wc%d" % hg, tag="wc", align_bytes=64)
+                wss[hg] = wcp.tile([P, 4, 512], U8, name="ws%d" % hg, tag="ws", align_bytes=64)
             nc.vector.quantize_mx(
-                out=wcs[ph][:, c, :].bitcast(FP8X4),
-                scales=wss[ph][:, c, :],
+                out=wcs[hg][:, c, :].bitcast(FP8X4),
+                scales=wss[hg][:, c, :],
                 in_=gws[i][:].rearrange("p w t -> p (w t)"),
             )
 
         accs = {}
 
-        def mx_pass(ph, j, c):
+        def mx_pass(hg, jj, c):
             if c == 0:
-                accs[(ph, j)] = mxp.tile([P, 512], F32, name="acc%d_%d" % (ph, j), tag="acc")
-            acc = accs[(ph, j)]
+                accs[(hg, jj)] = mxp.tile([P, 512], F32, name="acc%d_%d" % (hg, jj), tag="acc")
+            acc = accs[(hg, jj)]
             if c < 2:
                 rc, rs, g = xc, xs, c
             else:
                 rc, rs, g = hc, hs, c - 2
             nc.tensor.matmul_mx(
                 out=acc[:],
-                lhsT=wcs[ph][:, c, 128 * j : 128 * j + 128].bitcast(FP8X4),
-                lhsT_scale=wss[ph][:, c, 128 * j : 128 * j + 128],
+                lhsT=wcs[hg][:, c, 128 * jj : 128 * jj + 128].bitcast(FP8X4),
+                lhsT_scale=wss[hg][:, c, 128 * jj : 128 * jj + 128],
                 rhs=rc[:, 512 * g : 512 * g + 512].bitcast(FP8X4),
                 rhs_scale=rs[:, 512 * g : 512 * g + 512],
                 start=(c == 0),
                 stop=(c == 3),
             )
 
-        def pair_tiles(q):
-            return (2 * (q % 4), 2 * (q % 4) + 1)
-
-        def first_slot(q, c):
-            return max(0 if q < 2 else q + 1, 4 * (q // 4) + c)
-
-        def passes(s, fresh):
-            for q in range(12):
-                if (q >= 2 and q == s - 1) != fresh:
-                    continue
-                for c in range(4):
-                    if first_slot(q, c) == s:
-                        for j in pair_tiles(q):
-                            mx_pass(q // 4, j, c)
-
-        def bias_col(ph, j):
-            k = GATE_BIAS[ph] + j
+        def bias_col(gt, j):
+            k = GATE_BIAS[gt] + j
             return bcol[:, k : k + 1]
 
         def h_t(j):
@@ -186,19 +167,19 @@ def tile_yarnixcellv4_pa_kernel(
             return gh[:, 2048 * g : 2048 * g + 2048].rearrange("p (r t) -> p t r", t=4)[:, t, :]
 
         def add_transposed(bank, first, second):
-            for b in range(4):
-                cols = slice(128 * b, 128 * b + 128)
+            for k in range(8):
+                src = first if k < 4 else second
+                b = k % 4
                 nc.tensor.matmul(
-                    out=bank[:, b, :], lhsT=first[:, cols], rhs=ident_f[:], is_transpose=True, start=True, stop=False
-                )
-                nc.tensor.matmul(
-                    out=bank[:, b, :], lhsT=second[:, cols], rhs=ident_f[:], is_transpose=True, start=False, stop=True
+                    out=bank[:, b, :], lhsT=src[:, 128 * b : 128 * b + 128], rhs=ident_f[:],
+                    is_transpose=True, start=(k == 0), stop=(k == 7),
                 )
 
         out0_v = out_0.rearrange("(p b) u -> p b u", b=4)
         out1_v = out_1.rearrange("(p b) u -> p b u", b=4)
         banks = {}
         stages = {}
+        aps = {}
 
         def leave(kind, j, scale, out_v):
             if j % 2 == 0:
@@ -210,14 +191,64 @@ def tile_yarnixcellv4_pa_kernel(
                 u0 = 128 * (j - 1)
                 nc.sync.dma_start(out=out_v[:, :, u0 : u0 + 256], in_=st[:])
 
+        def angle_pair(p):
+            at = tpp.tile([P, 2, 512], BF16, name="at", tag="tp")
+            for j2 in range(2):
+                for b in range(4):
+                    k0 = b * 1024 + 128 * (2 * p + j2)
+                    nc.tensor.transpose(at[:, j2, 128 * b : 128 * b + 128], a_sb[:, k0 : k0 + 128], ident_b[:])
+            for j2 in range(2):
+                j = 2 * p + j2
+                ap = app.tile([P, 512], F32, name="ap", tag="ap")
+                nc.scalar.activation(out=ap[:], in_=at[:, j2, :], func=ACT.Copy, scale=persp[:, j : j + 1])
+                aps[j] = ap
+
+        def consume(hg):
+            gt = hg % 3
+            for jj in range(4):
+                j = 4 * (hg // 3) + jj
+                acc = accs[(hg, jj)]
+                if gt == 0:
+                    nc.scalar.activation(out=zt[:, j, :], in_=acc[:], func=ACT.Sigmoid, bias=bias_col(0, j), scale=1.0)
+                elif gt == 1:
+                    nc.scalar.activation(out=rt[:, j, :], in_=acc[:], func=ACT.Sigmoid, bias=bias_col(1, j), scale=1.0)
+                else:
+                    nc.vector.scalar_tensor_tensor(
+                        out=rt[:, j, :], in0=acc[:], scalar=bias_col(2, j), in1=rt[:, j, :], op0=ALU.add, op1=ALU.mult
+                    )
+                    nc.scalar.activation(out=rt[:, j, :], in_=rt[:, j, :], func=ACT.Tanh)
+
+        def second_stage(gt, j):
+            if gt == 0:
+                nc.vector.scalar_tensor_tensor(
+                    out=wt[:, j, :], in0=zt[:, j, :], scalar=1.0, in1=h_t(j), op0=ALU.subtract, op1=ALU.mult
+                )
+                bank = tpp.tile([P, 4, P], F32, name="pra", tag="tp")
+                add_transposed(bank, aps[j][:], zt[:, j, :])
+                banks[("ra", j)] = bank
+            elif gt == 2:
+                nc.vector.scalar_tensor_tensor(
+                    out=rt[:, j, :], in0=rt[:, j, :], scalar=-1.0, in1=zt[:, j, :], op0=ALU.mult, op1=ALU.mult
+                )
+                bank = tpp.tile([P, 4, P], F32, name="phb", tag="tp")
+                add_transposed(bank, wt[:, j, :], rt[:, j, :])
+                banks[("hb", j)] = bank
+
+        def third_stage(gt, j):
+            if gt == 0:
+                leave("ra", j, TWO_PI, out1_v)
+            elif gt == 2:
+                leave("hb", j, -1.0, out0_v)
+
+        load_rows(x_sb, x, 2)
+        load_rows(h_sb, h_state, 2)
         for k in range(RAW_BUFS):
             next_load()
 
-        gx = gwp.tile([P, 4096], BF16, name="gx", tag="gw", align_bytes=64)
-        xw = raws["x"][:].bitcast(F32)
+        xw = x_sb[:].bitcast(F32)
         gxw = gx[:].bitcast(F32)
-        for g in range(2):
-            for hf in range(2):
+        for hf in range(2):
+            for g in range(2):
                 xt = tpp.tile([P, 2, 256], F32, name="xt", tag="tp")
                 for u in range(2):
                     for b2 in range(2):
@@ -225,15 +256,13 @@ def tile_yarnixcellv4_pa_kernel(
                         nc.tensor.transpose(xt[:, u, 128 * b2 : 128 * b2 + 128], xw[:, w0 : w0 + 128], ident_f[:])
                 o0 = g * 1024 + hf * 512
                 copy_on(
-                    hf,
+                    g,
                     gxw[:, o0 : o0 + 512].rearrange("p (r u) -> p r u", u=2),
                     xt[:].rearrange("p u r -> p r u"),
                 )
-        next_load()
-        h_sb = raws["h"]
         hts = []
-        for g in range(2):
-            for hf in range(2):
+        for hf in range(2):
+            for g in range(2):
                 ht = tpp.tile([P, 4, 256], BF16, name="ht", tag="tp")
                 for t in range(4):
                     for b2 in range(2):
@@ -242,76 +271,33 @@ def tile_yarnixcellv4_pa_kernel(
                 hts.append(ht)
         nc.vector.quantize_mx(out=xc[:].bitcast(FP8X4), scales=xs[:], in_=gx[:])
         for k in range(4):
+            o0 = 2048 * (k % 2) + 1024 * (k // 2)
             copy_on(
                 k,
-                gh[:, 1024 * k : 1024 * k + 1024].rearrange("p (r t) -> p r t", t=4),
+                gh[:, o0 : o0 + 1024].rearrange("p (r t) -> p r t", t=4),
                 hts[k][:].rearrange("p t r -> p r t"),
             )
-        next_load()
         nc.vector.quantize_mx(out=hc[:].bitcast(FP8X4), scales=hs[:], in_=gh[:])
         pb = tpp.tile([P, P], BF16, name="pb", tag="tp")
         nc.tensor.transpose(pb[:], bp[:], ident_b[:])
         nc.vector.tensor_copy(out=bcol[:], in_=pb[:, 0:32])
         nc.vector.tensor_scalar_mul(out=persp[:], in0=bcol[:, 24:32], scalar1=1.0 / TWO_PI)
 
+        ANGLE_SLOTS = {2: 0, 3: 1, 13: 2, 14: 3}
         regroup(0)
-        for s in range(17):
-            if s < QUANT_FIRST and s <= 11:
+        for s in range(24 + 6):
+            if s < 24:
                 quant(s)
-            if s + 1 <= 11:
+            if s + 1 < 24:
                 regroup(s + 1)
-            if s >= QUANT_FIRST and s <= 11:
-                quant(s)
-            passes(s, False)
-            q2 = s - 5
-            if 0 <= q2 < 4:
-                for j in pair_tiles(q2):
-                    leave("ra", j, TWO_PI, out1_v)
-            q3 = s - 5
-            if 8 <= q3 < 12:
-                for j in pair_tiles(q3):
-                    leave("hb", j, -1.0, out0_v)
-            q1 = s - 4
-            if 0 <= q1 < 4:
-                for j in pair_tiles(q1):
-                    nc.vector.scalar_tensor_tensor(
-                        out=wt[:, j, :], in0=zt[:, j, :], scalar=1.0, in1=h_t(j), op0=ALU.subtract, op1=ALU.mult
-                    )
-            if 8 <= q1 < 12:
-                for j in pair_tiles(q1):
-                    nc.vector.scalar_tensor_tensor(
-                        out=rt[:, j, :], in0=rt[:, j, :], scalar=-1.0, in1=zt[:, j, :], op0=ALU.mult, op1=ALU.mult
-                    )
-                    bank = tpp.tile([P, 4, P], F32, name="phb", tag="tp")
-                    add_transposed(bank, rt[:, j, :], wt[:, j, :])
-                    banks[("hb", j)] = bank
-            q = s - 3
-            if 0 <= q < 4:
-                at = tpp.tile([P, 2, 512], BF16, name="at", tag="tp")
-                for j2 in range(2):
-                    for b in range(4):
-                        k0 = b * 1024 + 128 * (2 * q + j2)
-                        nc.tensor.transpose(at[:, j2, 128 * b : 128 * b + 128], a_sb[:, k0 : k0 + 128], ident_b[:])
-                for j in pair_tiles(q):
-                    nc.scalar.activation(
-                        out=zt[:, j, :], in_=accs[(0, j)][:], func=ACT.Sigmoid, bias=bias_col(0, j), scale=1.0
-                    )
-                for j in pair_tiles(q):
-                    ap = app.tile([P, 512], F32, name="ap", tag="ap")
-                    nc.scalar.activation(out=ap[:], in_=at[:, j % 2, :], func=ACT.Copy, scale=persp[:, j : j + 1])
-                    bank = tpp.tile([P, 4, P], F32, name="pra", tag="tp")
-                    add_transposed(bank, zt[:, j, :], ap[:])
-                    banks[("ra", j)] = bank
-            elif 4 <= q < 8:
-                for j in pair_tiles(q):
-                    nc.scalar.activation(
-                        out=rt[:, j, :], in_=accs[(1, j)][:], func=ACT.Sigmoid, bias=bias_col(1, j), scale=1.0
-                    )
-            elif 8 <= q < 12:
-                for j in pair_tiles(q):
-                    nc.vector.scalar_tensor_tensor(
-                        out=rt[:, j, :], in0=accs[(2, j)][:], scalar=bias_col(2, j), in1=rt[:, j, :],
-                        op0=ALU.add, op1=ALU.mult,
-                    )
-                    nc.scalar.activation(out=rt[:, j, :], in_=rt[:, j, :], func=ACT.Tanh)
-            passes(s, True)
+            if s < 24:
+                for jj in range(4):
+                    mx_pass(s // 4, jj, s % 4)
+            if s in ANGLE_SLOTS:
+                angle_pair(ANGLE_SLOTS[s])
+            for lag, stage in ((2, third_stage), (1, second_stage)):
+                v = s - 3 - lag
+                if 0 <= v < 24:
+                    stage((v // 4) % 3, 4 * (v // 12) + v % 4)
+            if s < 24 and s % 4 == 3:
+                consume(s // 4)

@@ -216,39 +216,49 @@ def tile_yarnixcellv4_pa_kernel(
                     nc.vector.scalar_tensor_tensor(
                         out=rt[:, j, :], in0=acc[:], scalar=bias_col(2, j), in1=rt[:, j, :], op0=ALU.add, op1=ALU.mult
                     )
-                    nc.scalar.activation(out=rt[:, j, :], in_=rt[:, j, :], func=ACT.Tanh)
+                    if jj % 2 == 1:
+                        nc.scalar.activation(out=rt[:, j - 1 : j + 1, :], in_=rt[:, j - 1 : j + 1, :], func=ACT.Tanh)
 
         def second_stage(gt, j):
             if gt == 0:
+                g, t = divmod(j, 4)
                 nc.vector.scalar_tensor_tensor(
-                    out=wt[:, j, :], in0=zt[:, j, :], scalar=1.0, in1=h_t(j), op0=ALU.subtract, op1=ALU.mult
+                    out=wt[:, j : j + 2, :], in0=zt[:, j : j + 2, :], scalar=1.0,
+                    in1=gh[:, 2048 * g : 2048 * g + 2048].rearrange("p (r t) -> p t r", t=4)[:, t : t + 2, :],
+                    op0=ALU.subtract, op1=ALU.mult,
                 )
-                bank = tpp.tile([P, 4, P], F32, name="pra", tag="tp")
-                add_transposed(bank, aps[j][:], zt[:, j, :])
-                banks[("ra", j)] = bank
+                for k in (j, j + 1):
+                    bank = tpp.tile([P, 4, P], F32, name="pra", tag="tp")
+                    add_transposed(bank, aps[k][:], zt[:, k, :])
+                    banks[("ra", k)] = bank
             elif gt == 2:
                 nc.vector.scalar_tensor_tensor(
-                    out=rt[:, j, :], in0=rt[:, j, :], scalar=-1.0, in1=zt[:, j, :], op0=ALU.mult, op1=ALU.mult
+                    out=rt[:, j : j + 2, :], in0=rt[:, j : j + 2, :], scalar=-1.0, in1=zt[:, j : j + 2, :],
+                    op0=ALU.mult, op1=ALU.mult,
                 )
-                bank = tpp.tile([P, 4, P], F32, name="phb", tag="tp")
-                add_transposed(bank, wt[:, j, :], rt[:, j, :])
-                banks[("hb", j)] = bank
+                for k in (j, j + 1):
+                    bank = tpp.tile([P, 4, P], F32, name="phb", tag="tp")
+                    add_transposed(bank, wt[:, k, :], rt[:, k, :])
+                    banks[("hb", k)] = bank
 
         def third_stage(gt, j):
-            if gt == 0:
-                leave("ra", j, TWO_PI, out1_v)
-            elif gt == 2:
-                leave("hb", j, -1.0, out0_v)
+            for k in (j, j + 1):
+                if gt == 0:
+                    leave("ra", k, TWO_PI, out1_v)
+                elif gt == 2:
+                    leave("hb", k, -1.0, out0_v)
 
+        for k in range(1):
+            next_load()
         load_rows(x_sb, x, 2)
         load_rows(h_sb, h_state, 2)
-        for k in range(RAW_BUFS):
+        for k in range(RAW_BUFS - 1):
             next_load()
 
         xw = x_sb[:].bitcast(F32)
         gxw = gx[:].bitcast(F32)
-        for hf in range(2):
-            for g in range(2):
+        for g in range(2):
+            for hf in range(2):
                 xt = tpp.tile([P, 2, 256], F32, name="xt", tag="tp")
                 for u in range(2):
                     for b2 in range(2):
@@ -256,28 +266,33 @@ def tile_yarnixcellv4_pa_kernel(
                         nc.tensor.transpose(xt[:, u, 128 * b2 : 128 * b2 + 128], xw[:, w0 : w0 + 128], ident_f[:])
                 o0 = g * 1024 + hf * 512
                 copy_on(
-                    g,
+                    hf,
                     gxw[:, o0 : o0 + 512].rearrange("p (r u) -> p r u", u=2),
                     xt[:].rearrange("p u r -> p r u"),
                 )
-        hts = []
-        for hf in range(2):
-            for g in range(2):
+            nc.vector.quantize_mx(
+                out=xc[:, 512 * g : 512 * g + 512].bitcast(FP8X4),
+                scales=xs[:, 512 * g : 512 * g + 512],
+                in_=gx[:, 2048 * g : 2048 * g + 2048],
+            )
+        for g in range(2):
+            for hf in range(2):
                 ht = tpp.tile([P, 4, 256], BF16, name="ht", tag="tp")
                 for t in range(4):
                     for b2 in range(2):
                         k0 = (2 * hf + b2) * 1024 + 512 * g + 128 * t
                         nc.tensor.transpose(ht[:, t, 128 * b2 : 128 * b2 + 128], h_sb[:, k0 : k0 + 128], ident_b[:])
-                hts.append(ht)
-        nc.vector.quantize_mx(out=xc[:].bitcast(FP8X4), scales=xs[:], in_=gx[:])
-        for k in range(4):
-            o0 = 2048 * (k % 2) + 1024 * (k // 2)
-            copy_on(
-                k,
-                gh[:, o0 : o0 + 1024].rearrange("p (r t) -> p r t", t=4),
-                hts[k][:].rearrange("p t r -> p r t"),
+                o0 = 2048 * g + 1024 * hf
+                copy_on(
+                    hf,
+                    gh[:, o0 : o0 + 1024].rearrange("p (r t) -> p r t", t=4),
+                    ht[:].rearrange("p t r -> p r t"),
+                )
+            nc.vector.quantize_mx(
+                out=hc[:, 512 * g : 512 * g + 512].bitcast(FP8X4),
+                scales=hs[:, 512 * g : 512 * g + 512],
+                in_=gh[:, 2048 * g : 2048 * g + 2048],
             )
-        nc.vector.quantize_mx(out=hc[:].bitcast(FP8X4), scales=hs[:], in_=gh[:])
         pb = tpp.tile([P, P], BF16, name="pb", tag="tp")
         nc.tensor.transpose(pb[:], bp[:], ident_b[:])
         nc.vector.tensor_copy(out=bcol[:], in_=pb[:, 0:32])
@@ -297,7 +312,7 @@ def tile_yarnixcellv4_pa_kernel(
                 angle_pair(ANGLE_SLOTS[s])
             for lag, stage in ((2, third_stage), (1, second_stage)):
                 v = s - 3 - lag
-                if 0 <= v < 24:
+                if 0 <= v < 24 and v % 2 == 0:
                     stage((v // 4) % 3, 4 * (v // 12) + v % 4)
             if s < 24 and s % 4 == 3:
                 consume(s // 4)

@@ -216,37 +216,29 @@ def tile_yarnixcellv4_pa_kernel(
                     nc.vector.scalar_tensor_tensor(
                         out=rt[:, j, :], in0=acc[:], scalar=bias_col(2, j), in1=rt[:, j, :], op0=ALU.add, op1=ALU.mult
                     )
-                    if jj % 2 == 1:
-                        nc.scalar.activation(out=rt[:, j - 1 : j + 1, :], in_=rt[:, j - 1 : j + 1, :], func=ACT.Tanh)
+                    nc.scalar.activation(out=rt[:, j, :], in_=rt[:, j, :], func=ACT.Tanh)
 
         def second_stage(gt, j):
             if gt == 0:
-                g, t = divmod(j, 4)
                 nc.vector.scalar_tensor_tensor(
-                    out=wt[:, j : j + 2, :], in0=zt[:, j : j + 2, :], scalar=1.0,
-                    in1=gh[:, 2048 * g : 2048 * g + 2048].rearrange("p (r t) -> p t r", t=4)[:, t : t + 2, :],
-                    op0=ALU.subtract, op1=ALU.mult,
+                    out=wt[:, j, :], in0=zt[:, j, :], scalar=1.0, in1=h_t(j), op0=ALU.subtract, op1=ALU.mult
                 )
-                for k in (j, j + 1):
-                    bank = tpp.tile([P, 4, P], F32, name="pra", tag="tp")
-                    add_transposed(bank, aps[k][:], zt[:, k, :])
-                    banks[("ra", k)] = bank
+                bank = tpp.tile([P, 4, P], F32, name="pra", tag="tp")
+                add_transposed(bank, aps[j][:], zt[:, j, :])
+                banks[("ra", j)] = bank
             elif gt == 2:
                 nc.vector.scalar_tensor_tensor(
-                    out=rt[:, j : j + 2, :], in0=rt[:, j : j + 2, :], scalar=-1.0, in1=zt[:, j : j + 2, :],
-                    op0=ALU.mult, op1=ALU.mult,
+                    out=rt[:, j, :], in0=rt[:, j, :], scalar=-1.0, in1=zt[:, j, :], op0=ALU.mult, op1=ALU.mult
                 )
-                for k in (j, j + 1):
-                    bank = tpp.tile([P, 4, P], F32, name="phb", tag="tp")
-                    add_transposed(bank, wt[:, k, :], rt[:, k, :])
-                    banks[("hb", k)] = bank
+                bank = tpp.tile([P, 4, P], F32, name="phb", tag="tp")
+                add_transposed(bank, wt[:, j, :], rt[:, j, :])
+                banks[("hb", j)] = bank
 
         def third_stage(gt, j):
-            for k in (j, j + 1):
-                if gt == 0:
-                    leave("ra", k, TWO_PI, out1_v)
-                elif gt == 2:
-                    leave("hb", k, -1.0, out0_v)
+            if gt == 0:
+                leave("ra", j, TWO_PI, out1_v)
+            elif gt == 2:
+                leave("hb", j, -1.0, out0_v)
 
         for k in range(1):
             next_load()
@@ -312,7 +304,7 @@ def tile_yarnixcellv4_pa_kernel(
                 angle_pair(ANGLE_SLOTS[s])
             for lag, stage in ((2, third_stage), (1, second_stage)):
                 v = s - 3 - lag
-                if 0 <= v < 24 and v % 2 == 0:
+                if 0 <= v < 24:
                     stage((v // 4) % 3, 4 * (v // 12) + v % 4)
             if s < 24 and s % 4 == 3:
                 consume(s // 4)

@@ -21,7 +21,7 @@ TWO_PI = 2.0 * math.pi
 GATE_COL = (1024, 0, 2048)
 GATE_BIAS = (8, 0, 16)
 AV_FIRST = 320
-AVS = (192, 320, 384)
+AVS = (192, 256, 384)
 
 
 def tile_yarnixcellv4_pa_kernel(
@@ -197,11 +197,7 @@ def tile_yarnixcellv4_pa_kernel(
                 for b in range(4):
                     k0 = b * 1024 + 128 * (2 * p + j2)
                     nc.tensor.transpose(at[:, j2, 128 * b : 128 * b + 128], a_sb[:, k0 : k0 + 128], ident_b[:])
-            for j2 in range(2):
-                j = 2 * p + j2
-                ap = app.tile([P, 512], F32, name="ap", tag="ap")
-                nc.scalar.activation(out=ap[:], in_=at[:, j2, :], func=ACT.Copy, scale=persp[:, j : j + 1])
-                aps[j] = ap
+                aps[2 * p + j2] = at[:, j2, :]
 
         def consume(hg):
             gt = hg % 3
@@ -223,8 +219,13 @@ def tile_yarnixcellv4_pa_kernel(
                 nc.vector.scalar_tensor_tensor(
                     out=wt[:, j, :], in0=zt[:, j, :], scalar=1.0, in1=h_t(j), op0=ALU.subtract, op1=ALU.mult
                 )
+                qt = app.tile([P, 512], F32, name="qt", tag="ap")
+                nc.vector.scalar_tensor_tensor(
+                    out=qt[:], in0=aps[j], scalar=persp[:, j : j + 1], in1=zt[:, j, :], op0=ALU.mult, op1=ALU.add
+                )
                 bank = tpp.tile([P, 4, P], F32, name="pra", tag="tp")
-                add_transposed(bank, aps[j][:], zt[:, j, :])
+                for b in range(4):
+                    nc.tensor.transpose(bank[:, b, :], qt[:, 128 * b : 128 * b + 128], ident_f[:])
                 banks[("ra", j)] = bank
             elif gt == 2:
                 nc.vector.scalar_tensor_tensor(
@@ -240,17 +241,15 @@ def tile_yarnixcellv4_pa_kernel(
             elif gt == 2:
                 leave("hb", j, -1.0, out0_v)
 
-        for k in range(1):
-            next_load()
         load_rows(x_sb, x, 2)
         load_rows(h_sb, h_state, 2)
-        for k in range(RAW_BUFS - 1):
+        for k in range(RAW_BUFS):
             next_load()
 
         xw = x_sb[:].bitcast(F32)
         gxw = gx[:].bitcast(F32)
-        for g in range(2):
-            for hf in range(2):
+        for hf in range(2):
+            for g in range(2):
                 xt = tpp.tile([P, 2, 256], F32, name="xt", tag="tp")
                 for u in range(2):
                     for b2 in range(2):
@@ -258,39 +257,34 @@ def tile_yarnixcellv4_pa_kernel(
                         nc.tensor.transpose(xt[:, u, 128 * b2 : 128 * b2 + 128], xw[:, w0 : w0 + 128], ident_f[:])
                 o0 = g * 1024 + hf * 512
                 copy_on(
-                    hf,
+                    g,
                     gxw[:, o0 : o0 + 512].rearrange("p (r u) -> p r u", u=2),
                     xt[:].rearrange("p u r -> p r u"),
                 )
-            nc.vector.quantize_mx(
-                out=xc[:, 512 * g : 512 * g + 512].bitcast(FP8X4),
-                scales=xs[:, 512 * g : 512 * g + 512],
-                in_=gx[:, 2048 * g : 2048 * g + 2048],
-            )
-        for g in range(2):
-            for hf in range(2):
+        hts = []
+        for hf in range(2):
+            for g in range(2):
                 ht = tpp.tile([P, 4, 256], BF16, name="ht", tag="tp")
                 for t in range(4):
                     for b2 in range(2):
                         k0 = (2 * hf + b2) * 1024 + 512 * g + 128 * t
                         nc.tensor.transpose(ht[:, t, 128 * b2 : 128 * b2 + 128], h_sb[:, k0 : k0 + 128], ident_b[:])
-                o0 = 2048 * g + 1024 * hf
-                copy_on(
-                    hf,
-                    gh[:, o0 : o0 + 1024].rearrange("p (r t) -> p r t", t=4),
-                    ht[:].rearrange("p t r -> p r t"),
-                )
-            nc.vector.quantize_mx(
-                out=hc[:, 512 * g : 512 * g + 512].bitcast(FP8X4),
-                scales=hs[:, 512 * g : 512 * g + 512],
-                in_=gh[:, 2048 * g : 2048 * g + 2048],
+                hts.append(ht)
+        nc.vector.quantize_mx(out=xc[:].bitcast(FP8X4), scales=xs[:], in_=gx[:])
+        for k in range(4):
+            o0 = 2048 * (k % 2) + 1024 * (k // 2)
+            copy_on(
+                k,
+                gh[:, o0 : o0 + 1024].rearrange("p (r t) -> p r t", t=4),
+                hts[k][:].rearrange("p t r -> p r t"),
             )
+        nc.vector.quantize_mx(out=hc[:].bitcast(FP8X4), scales=hs[:], in_=gh[:])
         pb = tpp.tile([P, P], BF16, name="pb", tag="tp")
         nc.tensor.transpose(pb[:], bp[:], ident_b[:])
         nc.vector.tensor_copy(out=bcol[:], in_=pb[:, 0:32])
         nc.vector.tensor_scalar_mul(out=persp[:], in0=bcol[:, 24:32], scalar1=1.0 / TWO_PI)
 
-        ANGLE_SLOTS = {2: 0, 3: 1, 13: 2, 14: 3}
+        ANGLE_SLOTS = {3: 0, 4: 1, 15: 2, 16: 3}
         regroup(0)
         for s in range(24 + 6):
             if s < 24:

@@ -13,15 +13,14 @@ U8 = mybir.dt.uint8
 FP8X4 = mybir.dt.float8_e4m3fn_x4
 ACT = mybir.ActivationFunctionType
 ALU = mybir.AluOpType
+PINNED = {mybir.EngineType.DVE, mybir.EngineType.Activation, mybir.EngineType.PE}
 
 P = 128
-PIN = False
-RAW_BUFS = 12
 TWO_PI = 2.0 * math.pi
 GATE_COL = (1024, 0, 2048)
 GATE_BIAS = (8, 0, 16)
-AV_FIRST = 320
-AVS = (192, 256, 384)
+AV_HEAD = 256
+AV = {2: 68, 3: 64, 4: 64, 5: 80}
 
 
 def tile_yarnixcellv4_pa_kernel(
@@ -29,17 +28,18 @@ def tile_yarnixcellv4_pa_kernel(
 ):
     nc = tc.nc
     with ExitStack() as ctx:
-        if PIN:
-            ctx.enter_context(tc.manual_schedule())
         const = ctx.enter_context(tc.tile_pool(name="const", bufs=1))
-        rawp = ctx.enter_context(tc.tile_pool(name="rawp", bufs=RAW_BUFS))
+        rawp = ctx.enter_context(tc.tile_pool(name="rawp", bufs=4))
         gwp = ctx.enter_context(tc.tile_pool(name="gwp", bufs=4))
-        wcp = ctx.enter_context(tc.tile_pool(name="wcp", bufs=3))
-        app = ctx.enter_context(tc.tile_pool(name="app", bufs=4))
-        stp = ctx.enter_context(tc.tile_pool(name="stp", bufs=3))
+        wcp = ctx.enter_context(tc.tile_pool(name="wcp", bufs=4))
+        eap = ctx.enter_context(tc.tile_pool(name="eap", bufs=5))
+        app = ctx.enter_context(tc.tile_pool(name="app", bufs=3))
+        stp = ctx.enter_context(tc.tile_pool(name="stp", bufs=2))
         mxp = ctx.enter_context(tc.psum_pool(name="mxp", bufs=4))
         tpp = ctx.enter_context(tc.psum_pool(name="tpp", bufs=4))
 
+        warm = const.tile([P, 1], F32, name="warm")
+        nc.vector.memset(warm[:], 0.0)
         ident_b = const.tile([P, P], BF16, name="ident_b")
         ident_f = const.tile([P, P], F32, name="ident_f")
         make_identity(nc, ident_f[:])
@@ -56,37 +56,37 @@ def tile_yarnixcellv4_pa_kernel(
         xs = const.tile([P, 1024], U8, name="xs", align_bytes=64)
         hc = const.tile([P, 1024], U32, name="hc", align_bytes=64)
         hs = const.tile([P, 1024], U8, name="hs", align_bytes=64)
-        zt = const.tile([P, 8, 512], F32, name="zt")
-        wt = const.tile([P, 8, 512], F32, name="wt")
-        rt = const.tile([P, 8, 512], F32, name="rt")
+        wch = [const.tile([P, 4, 512], U32, name="wch%d" % hg, align_bytes=64) for hg in range(2)]
+        wsh = [const.tile([P, 4, 512], U8, name="wsh%d" % hg, align_bytes=64) for hg in range(2)]
 
         nc.vector.memset(bp[:], 0.0)
         nc.scalar.dma_start(out=bp[0:24, :], in_=bias.rearrange("(r c) -> r c", c=P))
         nc.scalar.dma_start(out=bp[24:32, :], in_=persistence.rearrange("(r c) -> r c", c=P))
 
         raws = {}
+        gws = {}
         wcs = {}
         wss = {}
-        gws = {}
+        accs = {}
+        zts = {}
+        wts = {}
+        rts = {}
+        qts = {}
+        ahs = {}
+        banks = {}
+        stages = {}
 
-        def load_piece(i):
-            hg, c = divmod(i, 4)
+        def load_piece(hg, c):
+            if c == 0:
+                raws[hg] = rawp.tile([P, 4, 4, 512], BF16, name="raw%d" % hg, tag="raw")
             col = GATE_COL[hg % 3] + 512 * (hg // 3)
-            t = rawp.tile([P, 4, 512], BF16, name="raw%d" % i, tag="raw")
-            if c < 2:
-                for u in range(2):
-                    r0 = 512 * c + 256 * u
-                    nc.sync.dma_start(
-                        out=t[:, 2 * u : 2 * u + 2, :],
-                        in_=weight_ih[r0 : r0 + 256, col : col + 512].rearrange("(q e) w -> q e w", e=2),
-                    )
-            else:
-                r0 = 512 * (c - 2)
+            src = weight_ih if c < 2 else weight_hh
+            for u in range(2):
+                r0 = 512 * (c % 2) + 256 * u
                 nc.sync.dma_start(
-                    out=t[:],
-                    in_=weight_hh[r0 : r0 + 512, col : col + 512].rearrange("(t q) w -> q t w", q=P),
+                    out=raws[hg][:, c, 2 * u : 2 * u + 2, :],
+                    in_=src[r0 : r0 + 256, col : col + 512].rearrange("(q e) w -> q e w", e=2),
                 )
-            raws[i] = t
 
         def load_rows(t, src, pieces):
             tv = t[:].rearrange("p (b k) -> p b k", b=4)
@@ -95,65 +95,76 @@ def tile_yarnixcellv4_pa_kernel(
             for k in range(pieces):
                 nc.sync.dma_start(out=tv[:, n * k : n * k + n, :], in_=sv[:, n * k : n * k + n, :])
 
-        load_pos = [0]
-
-        def next_load():
-            k = load_pos[0]
-            if k >= 24:
-                return
-            load_pos[0] = k + 1
-            load_piece(k)
-            if k == 3:
-                load_rows(a_sb, local_angle, 1)
-
-        def copy_on(k, out, in_):
-            if k % 2 == 0:
+        def copy_on(on_scalar, out, in_):
+            if on_scalar:
                 nc.scalar.copy(out=out, in_=in_)
             else:
                 nc.vector.tensor_copy(out=out, in_=in_)
 
-        def regroup(i):
-            raw = raws[i]
-            av = AV_FIRST if i < 4 else AVS[(i // 4) % 3]
-            gw = gwp.tile([P, 512, 4], BF16, name="gw%d" % i, tag="gw", align_bytes=64)
+        def head_regroup(hg, c):
+            gw = gwp.tile([P, 512, 4], BF16, name="gwh%d_%d" % (hg, c), tag="gw", align_bytes=64)
             nc.vector.tensor_copy(
-                out=gw[:, 0:av, :].rearrange("p (c i) t -> p c t i", i=4),
-                in_=raw[:, :, 0:av].rearrange("p t (c i) -> p c t i", i=4),
+                out=gw[:, 0:AV_HEAD, :].rearrange("p (b i) t -> p b t i", i=4),
+                in_=raws[hg][:, c, :, 0:AV_HEAD].rearrange("p t (b i) -> p b t i", i=4),
             )
             nc.scalar.copy(
-                out=gw[:, av:512, :].rearrange("p (c i) t -> p c t i", i=4),
-                in_=raw[:, :, av:512].rearrange("p t (c i) -> p c t i", i=4),
+                out=gw[:, AV_HEAD:512, :].rearrange("p (b i) t -> p b t i", i=4),
+                in_=raws[hg][:, c, :, AV_HEAD:512].rearrange("p t (b i) -> p b t i", i=4),
             )
-            gws[i] = gw
-            next_load()
+            gws[("h", hg, c)] = gw
 
-        def quant(i):
-            hg, c = divmod(i, 4)
-            if c == 0:
-                wcs[hg] = wcp.tile([P, 4, 512], U32, name="wc%d" % hg, tag="wc", align_bytes=64)
-                wss[hg] = wcp.tile([P, 4, 512], U8, name="ws%d" % hg, tag="ws", align_bytes=64)
+        def head_quant(hg, c):
             nc.vector.quantize_mx(
-                out=wcs[hg][:, c, :].bitcast(FP8X4),
-                scales=wss[hg][:, c, :],
-                in_=gws[i][:].rearrange("p w t -> p (w t)"),
+                out=wch[hg][:, c, :].bitcast(FP8X4),
+                scales=wsh[hg][:, c, :],
+                in_=gws[("h", hg, c)][:].rearrange("p w t -> p (w t)"),
             )
 
-        accs = {}
+        def regroup_v(k):
+            hg, jj = divmod(k, 4)
+            av = AV[hg]
+            gws[k] = gwp.tile([P, 4, 128, 4], BF16, name="gw%d" % k, tag="gw", align_bytes=64)
+            nc.vector.tensor_copy(
+                out=gws[k][:, :, 0:av, :].rearrange("p c (b i) t -> p c b t i", i=4),
+                in_=raws[hg][:, :, :, 128 * jj : 128 * jj + av].rearrange("p c t (b i) -> p c b t i", i=4),
+            )
 
-        def mx_pass(hg, jj, c):
+        def regroup_s(k):
+            hg, jj = divmod(k, 4)
+            av = AV[hg]
+            nc.scalar.copy(
+                out=gws[k][:, :, av:128, :].rearrange("p c (b i) t -> p c b t i", i=4),
+                in_=raws[hg][:, :, :, 128 * jj + av : 128 * jj + 128].rearrange("p c t (b i) -> p c b t i", i=4),
+            )
+
+        def quant(k):
+            wcs[k] = wcp.tile([P, 4, 128], U32, name="wc%d" % k, tag="wc", align_bytes=64)
+            wss[k] = wcp.tile([P, 4, 128], U8, name="ws%d" % k, tag="ws", align_bytes=64)
+            nc.vector.quantize_mx(
+                out=wcs[k][:].rearrange("p c w -> p (c w)").bitcast(FP8X4),
+                scales=wss[k][:].rearrange("p c w -> p (c w)"),
+                in_=gws[k][:].rearrange("p c w t -> p (c w t)"),
+            )
+
+        def mx_pass(k, c):
             if c == 0:
-                accs[(hg, jj)] = mxp.tile([P, 512], F32, name="acc%d_%d" % (hg, jj), tag="acc")
-            acc = accs[(hg, jj)]
-            if c < 2:
-                rc, rs, g = xc, xs, c
+                accs[k] = mxp.tile([P, 512], F32, name="acc%d" % k, tag="acc")
+            multiply(accs[k][:], k, c, 0, 512)
+
+        def multiply(out, k, c, r0, rn):
+            if k < 8:
+                hg, jj = divmod(k, 4)
+                lw, ls = wch[hg][:, c, 128 * jj : 128 * jj + 128], wsh[hg][:, c, 128 * jj : 128 * jj + 128]
             else:
-                rc, rs, g = hc, hs, c - 2
+                lw, ls = wcs[k][:, c, :], wss[k][:, c, :]
+            rc, rs = (xc, xs) if c < 2 else (hc, hs)
+            r = 512 * (c % 2) + r0
             nc.tensor.matmul_mx(
-                out=acc[:],
-                lhsT=wcs[hg][:, c, 128 * jj : 128 * jj + 128].bitcast(FP8X4),
-                lhsT_scale=wss[hg][:, c, 128 * jj : 128 * jj + 128],
-                rhs=rc[:, 512 * g : 512 * g + 512].bitcast(FP8X4),
-                rhs_scale=rs[:, 512 * g : 512 * g + 512],
+                out=out,
+                lhsT=lw.bitcast(FP8X4),
+                lhsT_scale=ls,
+                rhs=rc[:, r : r + rn].bitcast(FP8X4),
+                rhs_scale=rs[:, r : r + rn],
                 start=(c == 0),
                 stop=(c == 3),
             )
@@ -162,143 +173,252 @@ def tile_yarnixcellv4_pa_kernel(
             k = GATE_BIAS[gt] + j
             return bcol[:, k : k + 1]
 
-        def h_t(j):
-            g, t = divmod(j, 4)
-            return gh[:, 2048 * g : 2048 * g + 2048].rearrange("p (r t) -> p t r", t=4)[:, t, :]
+        def kind(k):
+            hg, jj = divmod(k, 4)
+            return hg % 3, 4 * (hg // 3) + jj
 
-        def add_transposed(bank, first, second):
-            for k in range(8):
-                src = first if k < 4 else second
-                b = k % 4
-                nc.tensor.matmul(
-                    out=bank[:, b, :], lhsT=src[:, 128 * b : 128 * b + 128], rhs=ident_f[:],
-                    is_transpose=True, start=(k == 0), stop=(k == 7),
+        def gate_sigmoid(k):
+            gt, j = kind(k)
+            dst = zts if gt == 0 else rts
+            dst[j] = eap.tile([P, 512], F32, name="g%d" % k, tag="z" if gt == 0 else "r")
+            nc.scalar.activation(out=dst[j][:], in_=accs[k][:], func=ACT.Sigmoid, bias=bias_col(gt, j), scale=1.0)
+
+        def gate_n_v(k):
+            gt, j = kind(k)
+            nc.vector.scalar_tensor_tensor(
+                out=rts[j][:], in0=accs[k][:], scalar=bias_col(2, j), in1=rts[j][:], op0=ALU.add, op1=ALU.mult
+            )
+
+        def gate_n_s(k):
+            gt, j = kind(k)
+            nc.scalar.activation(out=rts[j][:], in_=rts[j][:], func=ACT.Tanh)
+
+        def transpose_ah(j):
+            ah = tpp.tile([P, 2, 512], BF16, name="ah", tag="tp")
+            for s, src in enumerate((a_sb, h_sb)):
+                for b in range(4):
+                    k0 = b * 1024 + 128 * j
+                    nc.tensor.transpose(ah[:, s, 128 * b : 128 * b + 128], src[:, k0 : k0 + 128], ident_b[:])
+            ahs[j] = ah
+
+        def second_v(k):
+            gt, j = kind(k)
+            if gt == 0:
+                wts[j] = eap.tile([P, 512], F32, name="w%d" % k, tag="w")
+                qts[j] = app.tile([P, 512], F32, name="q%d" % k, tag="q")
+                nc.vector.scalar_tensor_tensor(
+                    out=qts[j][:], in0=ahs[j][:, 0, :], scalar=persp[:, j : j + 1], in1=zts[j][:], op0=ALU.mult, op1=ALU.add
                 )
+                nc.vector.scalar_tensor_tensor(
+                    out=wts[j][:], in0=zts[j][:], scalar=1.0, in1=ahs[j][:, 1, :], op0=ALU.subtract, op1=ALU.mult
+                )
+            elif gt == 2:
+                nc.vector.scalar_tensor_tensor(
+                    out=rts[j][:], in0=rts[j][:], scalar=-1.0, in1=zts[j][:], op0=ALU.mult, op1=ALU.mult
+                )
+
+        def second_t(k):
+            gt, j = kind(k)
+            if gt == 0:
+                bank = tpp.tile([P, 4, P], F32, name="pra", tag="tp")
+                for b in range(4):
+                    nc.tensor.transpose(bank[:, b, :], qts[j][:, 128 * b : 128 * b + 128], ident_f[:])
+                banks[k] = bank
+            elif gt == 2:
+                bank = tpp.tile([P, 4, P], F32, name="phb", tag="tp")
+                for i in range(8):
+                    src = wts[j] if i < 4 else rts[j]
+                    b = i % 4
+                    nc.tensor.matmul(
+                        out=bank[:, b, :], lhsT=src[:, 128 * b : 128 * b + 128], rhs=ident_f[:],
+                        is_transpose=True, start=(i == 0), stop=(i == 7),
+                    )
+                banks[k] = bank
 
         out0_v = out_0.rearrange("(p b) u -> p b u", b=4)
         out1_v = out_1.rearrange("(p b) u -> p b u", b=4)
-        banks = {}
-        stages = {}
-        aps = {}
 
-        def leave(kind, j, scale, out_v):
+        def leave(k):
+            gt, j = kind(k)
+            if gt == 1:
+                return
             if j % 2 == 0:
-                stages[kind] = stp.tile([P, 4, 256], F32, name="st_%s" % kind, tag=kind)
-            st = stages[kind]
+                stages[gt] = stp.tile([P, 4, 256], F32, name="st%d" % gt, tag="st%d" % gt)
+            st = stages[gt]
             o = 128 * (j % 2)
-            nc.scalar.activation(out=st[:, :, o : o + 128], in_=banks[(kind, j)][:], func=ACT.Copy, scale=scale)
-            if j % 2 == 1:
+            nc.scalar.activation(
+                out=st[:, :, o : o + 128], in_=banks[k][:], func=ACT.Copy, scale=TWO_PI if gt == 0 else -1.0
+            )
+            if k == 22:
+                nc.sync.dma_start(out=out0_v[:, :, 768:896], in_=st[:, :, 0:128])
+            elif j % 2 == 1:
                 u0 = 128 * (j - 1)
-                nc.sync.dma_start(out=out_v[:, :, u0 : u0 + 256], in_=st[:])
+                nc.sync.dma_start(out=(out1_v if gt == 0 else out0_v)[:, :, u0 : u0 + 256], in_=st[:])
 
-        def angle_pair(p):
-            at = tpp.tile([P, 2, 512], BF16, name="at", tag="tp")
-            for j2 in range(2):
-                for b in range(4):
-                    k0 = b * 1024 + 128 * (2 * p + j2)
-                    nc.tensor.transpose(at[:, j2, 128 * b : 128 * b + 128], a_sb[:, k0 : k0 + 128], ident_b[:])
-                aps[2 * p + j2] = at[:, j2, :]
+        last = {}
 
-        def consume(hg):
-            gt = hg % 3
-            for jj in range(4):
-                j = 4 * (hg // 3) + jj
-                acc = accs[(hg, jj)]
-                if gt == 0:
-                    nc.scalar.activation(out=zt[:, j, :], in_=acc[:], func=ACT.Sigmoid, bias=bias_col(0, j), scale=1.0)
-                elif gt == 1:
-                    nc.scalar.activation(out=rt[:, j, :], in_=acc[:], func=ACT.Sigmoid, bias=bias_col(1, j), scale=1.0)
-                else:
-                    nc.vector.scalar_tensor_tensor(
-                        out=rt[:, j, :], in0=acc[:], scalar=bias_col(2, j), in1=rt[:, j, :], op0=ALU.add, op1=ALU.mult
-                    )
-                    nc.scalar.activation(out=rt[:, j, :], in_=rt[:, j, :], func=ACT.Tanh)
+        def last_mx(i):
+            last[i] = mxp.tile([P, 512], F32, name="last%d" % i, tag="acc")
+            for c in range(4):
+                multiply(last[i][:, 0:256], 23, c, 256 * i, 256)
 
-        def second_stage(gt, j):
-            if gt == 0:
-                nc.vector.scalar_tensor_tensor(
-                    out=wt[:, j, :], in0=zt[:, j, :], scalar=1.0, in1=h_t(j), op0=ALU.subtract, op1=ALU.mult
+        def last_half(i):
+            rt = rts[7][:, 256 * i : 256 * i + 256]
+            zt = zts[7][:, 256 * i : 256 * i + 256]
+            nc.vector.scalar_tensor_tensor(
+                out=rt, in0=last[i][:, 0:256], scalar=bias_col(2, 7), in1=rt, op0=ALU.add, op1=ALU.mult
+            )
+            nc.scalar.activation(out=rt, in_=rt, func=ACT.Tanh)
+
+        def last_half2(i):
+            rt = rts[7][:, 256 * i : 256 * i + 256]
+            zt = zts[7][:, 256 * i : 256 * i + 256]
+            nc.vector.scalar_tensor_tensor(out=rt, in0=rt, scalar=-1.0, in1=zt, op0=ALU.mult, op1=ALU.mult)
+            bank = tpp.tile([P, 2, P], F32, name="plast", tag="tp")
+            for q in range(4):
+                src = wts[7] if q < 2 else rts[7]
+                b = 2 * i + q % 2
+                nc.tensor.matmul(
+                    out=bank[:, q % 2, :], lhsT=src[:, 128 * b : 128 * b + 128], rhs=ident_f[:],
+                    is_transpose=True, start=(q == 0), stop=(q == 3),
                 )
-                qt = app.tile([P, 512], F32, name="qt", tag="ap")
-                nc.vector.scalar_tensor_tensor(
-                    out=qt[:], in0=aps[j], scalar=persp[:, j : j + 1], in1=zt[:, j, :], op0=ALU.mult, op1=ALU.add
-                )
-                bank = tpp.tile([P, 4, P], F32, name="pra", tag="tp")
-                for b in range(4):
-                    nc.tensor.transpose(bank[:, b, :], qt[:, 128 * b : 128 * b + 128], ident_f[:])
-                banks[("ra", j)] = bank
-            elif gt == 2:
-                nc.vector.scalar_tensor_tensor(
-                    out=rt[:, j, :], in0=rt[:, j, :], scalar=-1.0, in1=zt[:, j, :], op0=ALU.mult, op1=ALU.mult
-                )
-                bank = tpp.tile([P, 4, P], F32, name="phb", tag="tp")
-                add_transposed(bank, wt[:, j, :], rt[:, j, :])
-                banks[("hb", j)] = bank
-
-        def third_stage(gt, j):
-            if gt == 0:
-                leave("ra", j, TWO_PI, out1_v)
-            elif gt == 2:
-                leave("hb", j, -1.0, out0_v)
+            st = stp.tile([P, 2, P], F32, name="stl%d" % i, tag="stl")
+            nc.scalar.activation(out=st[:], in_=bank[:], func=ACT.Copy, scale=-1.0)
+            nc.sync.dma_start(out=out0_v[:, 2 * i : 2 * i + 2, 896:1024], in_=st[:])
 
         load_rows(x_sb, x, 2)
+        load_piece(0, 0)
+        load_piece(0, 1)
         load_rows(h_sb, h_state, 2)
-        for k in range(RAW_BUFS):
-            next_load()
+        load_piece(0, 2)
+        load_piece(0, 3)
+        load_piece(1, 0)
+        load_piece(1, 1)
+        load_piece(1, 2)
+        av4 = a_sb[:].rearrange("p (b k) -> p b k", b=4)
+        as4 = local_angle.rearrange("(p b) k -> p b k", b=4)
+        nc.sync.dma_start(out=av4[:, :, 0:512], in_=as4[:, :, 0:512])
+        load_piece(1, 3)
+        for c in range(4):
+            load_piece(2, c)
+        nc.sync.dma_start(out=av4[:, :, 512:1024], in_=as4[:, :, 512:1024])
+        for hg in range(3, 6):
+            for c in range(4):
+                load_piece(hg, c)
 
-        xw = x_sb[:].bitcast(F32)
-        gxw = gx[:].bitcast(F32)
-        for hf in range(2):
-            for g in range(2):
-                xt = tpp.tile([P, 2, 256], F32, name="xt", tag="tp")
-                for u in range(2):
-                    for b2 in range(2):
-                        w0 = (2 * hf + b2) * 512 + 256 * g + 128 * u
-                        nc.tensor.transpose(xt[:, u, 128 * b2 : 128 * b2 + 128], xw[:, w0 : w0 + 128], ident_f[:])
-                o0 = g * 1024 + hf * 512
-                copy_on(
-                    g,
-                    gxw[:, o0 : o0 + 512].rearrange("p (r u) -> p r u", u=2),
-                    xt[:].rearrange("p u r -> p r u"),
-                )
-        hts = []
-        for hf in range(2):
-            for g in range(2):
-                ht = tpp.tile([P, 4, 256], BF16, name="ht", tag="tp")
-                for t in range(4):
-                    for b2 in range(2):
-                        k0 = (2 * hf + b2) * 1024 + 512 * g + 128 * t
-                        nc.tensor.transpose(ht[:, t, 128 * b2 : 128 * b2 + 128], h_sb[:, k0 : k0 + 128], ident_b[:])
-                hts.append(ht)
-        nc.vector.quantize_mx(out=xc[:].bitcast(FP8X4), scales=xs[:], in_=gx[:])
-        for k in range(4):
-            o0 = 2048 * (k % 2) + 1024 * (k // 2)
+        def word_transpose(src, hf, g):
+            xt = tpp.tile([P, 2, 256], F32, name="xt", tag="tp")
+            sw = src[:].bitcast(F32)
+            for u in range(2):
+                for b2 in range(2):
+                    w0 = (2 * hf + b2) * 512 + 256 * g + 128 * u
+                    nc.tensor.transpose(xt[:, u, 128 * b2 : 128 * b2 + 128], sw[:, w0 : w0 + 128], ident_f[:])
+            return xt
+
+        def word_leave(dst, hf, g, xt, on_scalar):
+            o0 = g * 1024 + hf * 512
             copy_on(
-                k,
-                gh[:, o0 : o0 + 1024].rearrange("p (r t) -> p r t", t=4),
-                hts[k][:].rearrange("p t r -> p r t"),
+                on_scalar,
+                dst[:].bitcast(F32)[:, o0 : o0 + 512].rearrange("p (r u) -> p r u", u=2),
+                xt[:].rearrange("p u r -> p r u"),
             )
-        nc.vector.quantize_mx(out=hc[:].bitcast(FP8X4), scales=hs[:], in_=gh[:])
-        pb = tpp.tile([P, P], BF16, name="pb", tag="tp")
-        nc.tensor.transpose(pb[:], bp[:], ident_b[:])
-        nc.vector.tensor_copy(out=bcol[:], in_=pb[:, 0:32])
-        nc.vector.tensor_scalar_mul(out=persp[:], in0=bcol[:, 24:32], scalar1=1.0 / TWO_PI)
 
-        ANGLE_SLOTS = {3: 0, 4: 1, 15: 2, 16: 3}
-        regroup(0)
-        for s in range(24 + 6):
-            if s < 24:
-                quant(s)
-            if s + 1 < 24:
-                regroup(s + 1)
-            if s < 24:
-                for jj in range(4):
-                    mx_pass(s // 4, jj, s % 4)
-            if s in ANGLE_SLOTS:
-                angle_pair(ANGLE_SLOTS[s])
-            for lag, stage in ((2, third_stage), (1, second_stage)):
-                v = s - 3 - lag
-                if 0 <= v < 24:
-                    stage((v // 4) % 3, 4 * (v // 12) + v % 4)
-            if s < 24 and s % 4 == 3:
-                consume(s // 4)
+        def sig_step(k):
+            return k + 1
+
+        def second_step(k):
+            return k + 2 if k >= 4 else k + 3
+
+        def r_step(k):
+            return k - 3 if k < 16 else k - 2
+
+        with tc.manual_schedule(engines=PINNED):
+            nc.scalar.activation(out=warm[:], in_=warm[:], func=ACT.Sigmoid)
+            for hf in range(2):
+                for g in range(2):
+                    xt = word_transpose(x_sb, hf, g)
+                    word_leave(gx, hf, g, xt, g == 1)
+            head_regroup(0, 0)
+            nc.vector.quantize_mx(out=xc[:].bitcast(FP8X4), scales=xs[:], in_=gx[:])
+            pb = tpp.tile([P, P], BF16, name="pb", tag="tp")
+            nc.tensor.transpose(pb[:], bp[:], ident_b[:])
+            head_regroup(0, 1)
+            head_quant(0, 0)
+            nc.vector.tensor_copy(out=bcol[:], in_=pb[:, 0:32])
+            head_quant(0, 1)
+            nc.vector.tensor_scalar_mul(out=persp[:], in0=bcol[:, 24:32], scalar1=1.0 / TWO_PI)
+            for hf in range(2):
+                for g in range(2):
+                    xt = word_transpose(h_sb, hf, g)
+                    word_leave(gh, hf, g, xt, True)
+            for c in range(2):
+                for k in range(4):
+                    mx_pass(k, c)
+            head_regroup(0, 2)
+            nc.vector.quantize_mx(out=hc[:].bitcast(FP8X4), scales=hs[:], in_=gh[:])
+            head_regroup(0, 3)
+            head_quant(0, 2)
+            for k in range(4):
+                mx_pass(k, 2)
+            head_regroup(1, 0)
+            head_quant(0, 3)
+            for k in range(4):
+                mx_pass(k, 3)
+            head_regroup(1, 1)
+            head_quant(1, 0)
+            gate_sigmoid(0)
+            head_regroup(1, 2)
+            head_quant(1, 1)
+            gate_sigmoid(1)
+            transpose_ah(0)
+            head_quant(1, 2)
+            second_v(0)
+            head_regroup(1, 3)
+            gate_sigmoid(2)
+            second_t(0)
+            transpose_ah(1)
+            second_v(1)
+            head_quant(1, 3)
+
+            for s in range(4, 27):
+                if s < 23:
+                    for c in range(4):
+                        mx_pass(s, c)
+                elif s == 23:
+                    last_mx(0)
+                    last_mx(1)
+                for k in range(4, 23):
+                    if sig_step(k) == s and kind(k)[0] == 2:
+                        gate_n_v(k)
+                for k in range(2, 23):
+                    if second_step(k) == s:
+                        second_v(k)
+                for k in range(8, 24):
+                    if r_step(k) + 1 == s:
+                        quant(k)
+                for k in range(8, 24):
+                    if r_step(k) == s:
+                        regroup_v(k)
+                for k in range(1, 23):
+                    if second_step(k) == s:
+                        second_t(k)
+                    if second_step(k) == s + 1 and kind(k)[0] == 0 and k != 1:
+                        transpose_ah(kind(k)[1])
+                for k in range(22):
+                    if second_step(k) == s - 1:
+                        leave(k)
+                for k in range(3, 23):
+                    if sig_step(k) == s:
+                        if kind(k)[0] == 2:
+                            gate_n_s(k)
+                        else:
+                            gate_sigmoid(k)
+                for k in range(8, 24):
+                    if r_step(k) == s:
+                        regroup_s(k)
+                if s == 24:
+                    last_half(0)
+                    last_half(1)
+                    leave(22)
+                    last_half2(0)
+                    last_half2(1)

@@ -327,10 +327,16 @@ def tile_yarnixcellv4_pa_kernel(
             return k + 1
 
         def second_step(k):
-            return k + 2 if k >= 4 else k + 3
+            return k + 2 if k >= 4 else k + 4
+
+        def turn_step(k):
+            return second_step(k) + (0 if k < 22 else 0)
+
+        def leave_step(k):
+            return turn_step(k) + 1
 
         def r_step(k):
-            return k - 3 if k < 16 else k - 2
+            return k - 3 if k < 20 else k - 2
 
         with tc.manual_schedule(engines=PINNED):
             nc.scalar.activation(out=warm[:], in_=warm[:], func=ACT.Sigmoid)
@@ -371,26 +377,26 @@ def tile_yarnixcellv4_pa_kernel(
             head_quant(1, 1)
             gate_sigmoid(1)
             transpose_ah(0)
-            head_quant(1, 2)
-            second_v(0)
-            head_regroup(1, 3)
-            gate_sigmoid(2)
-            second_t(0)
             transpose_ah(1)
-            second_v(1)
+            head_regroup(1, 3)
+            head_quant(1, 2)
+            gate_sigmoid(2)
             head_quant(1, 3)
 
-            for s in range(4, 27):
+            for s in range(4, 28):
                 if s < 23:
                     for c in range(4):
                         mx_pass(s, c)
                 elif s == 23:
                     last_mx(0)
                     last_mx(1)
+                for k in range(2, 23):
+                    if second_step(k) == s + 1 and kind(k)[0] == 0:
+                        transpose_ah(kind(k)[1])
                 for k in range(4, 23):
                     if sig_step(k) == s and kind(k)[0] == 2:
                         gate_n_v(k)
-                for k in range(2, 23):
+                for k in range(0, 23):
                     if second_step(k) == s:
                         second_v(k)
                 for k in range(8, 24):
@@ -399,13 +405,11 @@ def tile_yarnixcellv4_pa_kernel(
                 for k in range(8, 24):
                     if r_step(k) == s:
                         regroup_v(k)
-                for k in range(1, 23):
-                    if second_step(k) == s:
+                for k in range(23):
+                    if turn_step(k) == s:
                         second_t(k)
-                    if second_step(k) == s + 1 and kind(k)[0] == 0 and k != 1:
-                        transpose_ah(kind(k)[1])
                 for k in range(22):
-                    if second_step(k) == s - 1:
+                    if leave_step(k) == s:
                         leave(k)
                 for k in range(3, 23):
                     if sig_step(k) == s:

@@ -19,8 +19,8 @@ P = 128
 TWO_PI = 2.0 * math.pi
 GATE_COL = (1024, 0, 2048)
 GATE_BIAS = (8, 0, 16)
-AV_HEAD = 256
-AV = {2: 68, 3: 64, 4: 64, 5: 80}
+AV_HEAD = (288, 320)
+AV = {2: 64, 3: 64, 4: 64, 5: 80}
 
 
 def tile_yarnixcellv4_pa_kernel(
@@ -104,12 +104,12 @@ def tile_yarnixcellv4_pa_kernel(
         def head_regroup(hg, c):
             gw = gwp.tile([P, 512, 4], BF16, name="gwh%d_%d" % (hg, c), tag="gw", align_bytes=64)
             nc.vector.tensor_copy(
-                out=gw[:, 0:AV_HEAD, :].rearrange("p (b i) t -> p b t i", i=4),
-                in_=raws[hg][:, c, :, 0:AV_HEAD].rearrange("p t (b i) -> p b t i", i=4),
+                out=gw[:, 0 : AV_HEAD[hg], :].rearrange("p (b i) t -> p b t i", i=4),
+                in_=raws[hg][:, c, :, 0 : AV_HEAD[hg]].rearrange("p t (b i) -> p b t i", i=4),
             )
             nc.scalar.copy(
-                out=gw[:, AV_HEAD:512, :].rearrange("p (b i) t -> p b t i", i=4),
-                in_=raws[hg][:, c, :, AV_HEAD:512].rearrange("p t (b i) -> p b t i", i=4),
+                out=gw[:, AV_HEAD[hg] : 512, :].rearrange("p (b i) t -> p b t i", i=4),
+                in_=raws[hg][:, c, :, AV_HEAD[hg] : 512].rearrange("p t (b i) -> p b t i", i=4),
             )
             gws[("h", hg, c)] = gw
 
@@ -262,18 +262,22 @@ def tile_yarnixcellv4_pa_kernel(
             for c in range(4):
                 multiply(last[i][:, 0:256], 23, c, 256 * i, 256)
 
-        def last_half(i):
+        def last_v(i):
             rt = rts[7][:, 256 * i : 256 * i + 256]
-            zt = zts[7][:, 256 * i : 256 * i + 256]
             nc.vector.scalar_tensor_tensor(
                 out=rt, in0=last[i][:, 0:256], scalar=bias_col(2, 7), in1=rt, op0=ALU.add, op1=ALU.mult
             )
+
+        def last_s(i):
+            rt = rts[7][:, 256 * i : 256 * i + 256]
             nc.scalar.activation(out=rt, in_=rt, func=ACT.Tanh)
 
-        def last_half2(i):
+        def last_v2(i):
             rt = rts[7][:, 256 * i : 256 * i + 256]
             zt = zts[7][:, 256 * i : 256 * i + 256]
             nc.vector.scalar_tensor_tensor(out=rt, in0=rt, scalar=-1.0, in1=zt, op0=ALU.mult, op1=ALU.mult)
+
+        def last_t(i):
             bank = tpp.tile([P, 2, P], F32, name="plast", tag="tp")
             for q in range(4):
                 src = wts[7] if q < 2 else rts[7]
@@ -282,8 +286,14 @@ def tile_yarnixcellv4_pa_kernel(
                     out=bank[:, q % 2, :], lhsT=src[:, 128 * b : 128 * b + 128], rhs=ident_f[:],
                     is_transpose=True, start=(q == 0), stop=(q == 3),
                 )
+            banks[("last", i)] = bank
+
+        def last_leave(i):
             st = stp.tile([P, 2, P], F32, name="stl%d" % i, tag="stl")
-            nc.scalar.activation(out=st[:], in_=bank[:], func=ACT.Copy, scale=-1.0)
+            if i == 0:
+                nc.scalar.activation(out=st[:], in_=banks[("last", i)][:], func=ACT.Copy, scale=-1.0)
+            else:
+                nc.vector.tensor_scalar_mul(out=st[:], in0=banks[("last", i)][:], scalar1=-1.0)
             nc.sync.dma_start(out=out0_v[:, 2 * i : 2 * i + 2, 896:1024], in_=st[:])
 
         load_rows(x_sb, x, 2)
@@ -326,17 +336,28 @@ def tile_yarnixcellv4_pa_kernel(
         def sig_step(k):
             return k + 1
 
+        def stt_step(k):
+            return k + 1
+
+        def tanh_step(k):
+            return k + 1
+
         def second_step(k):
-            return k + 2 if k >= 4 else k + 4
+            if k < 4:
+                return k + 4
+            return k + (2 if kind(k)[0] == 0 else 2)
 
         def turn_step(k):
-            return second_step(k) + (0 if k < 22 else 0)
+            return second_step(k) + 1
 
         def leave_step(k):
             return turn_step(k) + 1
 
         def r_step(k):
-            return k - 3 if k < 20 else k - 2
+            return k - 4
+
+        def q_step(k):
+            return r_step(k) + 2
 
         with tc.manual_schedule(engines=PINNED):
             nc.scalar.activation(out=warm[:], in_=warm[:], func=ACT.Sigmoid)
@@ -383,46 +404,69 @@ def tile_yarnixcellv4_pa_kernel(
             gate_sigmoid(2)
             head_quant(1, 3)
 
-            for s in range(4, 28):
-                if s < 23:
-                    for c in range(4):
-                        mx_pass(s, c)
-                elif s == 23:
-                    last_mx(0)
-                    last_mx(1)
-                for k in range(2, 23):
+            for s in range(4, 23):
+                for c in range(4):
+                    mx_pass(s, c)
+                for k in range(2, 22):
                     if second_step(k) == s + 1 and kind(k)[0] == 0:
                         transpose_ah(kind(k)[1])
-                for k in range(4, 23):
-                    if sig_step(k) == s and kind(k)[0] == 2:
+                for k in range(22):
+                    if turn_step(k) == s:
+                        second_t(k)
+                for k in range(4, 22):
+                    if stt_step(k) == s and kind(k)[0] == 2:
                         gate_n_v(k)
-                for k in range(0, 23):
+                for k in range(22):
                     if second_step(k) == s:
                         second_v(k)
                 for k in range(8, 24):
-                    if r_step(k) + 1 == s:
+                    if q_step(k) == s:
                         quant(k)
                 for k in range(8, 24):
                     if r_step(k) == s:
                         regroup_v(k)
-                for k in range(23):
-                    if turn_step(k) == s:
-                        second_t(k)
                 for k in range(22):
                     if leave_step(k) == s:
                         leave(k)
-                for k in range(3, 23):
-                    if sig_step(k) == s:
-                        if kind(k)[0] == 2:
-                            gate_n_s(k)
-                        else:
-                            gate_sigmoid(k)
+                for k in range(3, 22):
+                    if sig_step(k) == s and kind(k)[0] != 2:
+                        gate_sigmoid(k)
+                    if tanh_step(k) == s and kind(k)[0] == 2:
+                        gate_n_s(k)
                 for k in range(8, 24):
                     if r_step(k) == s:
                         regroup_s(k)
-                if s == 24:
-                    last_half(0)
-                    last_half(1)
-                    leave(22)
-                    last_half2(0)
-                    last_half2(1)
+            last_mx(0)
+            last_mx(1)
+            for k in range(20, 22):
+                if turn_step(k) > 22 and second_step(k) <= 22:
+                    second_t(k)
+            for k in range(20, 23):
+                if stt_step(k) > 22:
+                    gate_n_v(k)
+            for i in range(2):
+                last_v(i)
+            for k in range(18, 22):
+                if second_step(k) > 22:
+                    second_v(k)
+            for k in range(18, 22):
+                if leave_step(k) > 22 and turn_step(k) <= 22:
+                    leave(k)
+            for k in range(20, 23):
+                if tanh_step(k) > 22:
+                    gate_n_s(k)
+            for i in range(2):
+                last_s(i)
+            for k in range(18, 22):
+                if second_step(k) > 22:
+                    second_t(k)
+            second_v(22)
+            second_t(22)
+            for k in range(18, 22):
+                if turn_step(k) > 22:
+                    leave(k)
+            leave(22)
+            for i in range(2):
+                last_v2(i)
+                last_t(i)
+                last_leave(i)

@@ -20,7 +20,7 @@ TWO_PI = 2.0 * math.pi
 GATE_COL = (1024, 0, 2048)
 GATE_BIAS = (8, 0, 16)
 AV_HEAD = (288, 320)
-AV = {2: 64, 3: 64, 4: 64, 5: 80}
+AV = {2: 72, 3: 64, 4: 72, 5: 72}
 
 
 def tile_yarnixcellv4_pa_kernel(
@@ -104,12 +104,12 @@ def tile_yarnixcellv4_pa_kernel(
         def head_regroup(hg, c):
             gw = gwp.tile([P, 512, 4], BF16, name="gwh%d_%d" % (hg, c), tag="gw", align_bytes=64)
             nc.vector.tensor_copy(
-                out=gw[:, 0 : AV_HEAD[hg], :].rearrange("p (b i) t -> p b t i", i=4),
-                in_=raws[hg][:, c, :, 0 : AV_HEAD[hg]].rearrange("p t (b i) -> p b t i", i=4),
+                out=gw[:, 0 : AV_HEAD[hg], :].rearrange("p (b i) t -> p b t i", i=8),
+                in_=raws[hg][:, c, :, 0 : AV_HEAD[hg]].rearrange("p t (b i) -> p b t i", i=8),
             )
             nc.scalar.copy(
-                out=gw[:, AV_HEAD[hg] : 512, :].rearrange("p (b i) t -> p b t i", i=4),
-                in_=raws[hg][:, c, :, AV_HEAD[hg] : 512].rearrange("p t (b i) -> p b t i", i=4),
+                out=gw[:, AV_HEAD[hg] : 512, :].rearrange("p (b i) t -> p b t i", i=8),
+                in_=raws[hg][:, c, :, AV_HEAD[hg] : 512].rearrange("p t (b i) -> p b t i", i=8),
             )
             gws[("h", hg, c)] = gw
 
@@ -125,16 +125,16 @@ def tile_yarnixcellv4_pa_kernel(
             av = AV[hg]
             gws[k] = gwp.tile([P, 4, 128, 4], BF16, name="gw%d" % k, tag="gw", align_bytes=64)
             nc.vector.tensor_copy(
-                out=gws[k][:, :, 0:av, :].rearrange("p c (b i) t -> p c b t i", i=4),
-                in_=raws[hg][:, :, :, 128 * jj : 128 * jj + av].rearrange("p c t (b i) -> p c b t i", i=4),
+                out=gws[k][:, :, 0:av, :].rearrange("p c (b i) t -> p c b t i", i=8),
+                in_=raws[hg][:, :, :, 128 * jj : 128 * jj + av].rearrange("p c t (b i) -> p c b t i", i=8),
             )
 
         def regroup_s(k):
             hg, jj = divmod(k, 4)
             av = AV[hg]
             nc.scalar.copy(
-                out=gws[k][:, :, av:128, :].rearrange("p c (b i) t -> p c b t i", i=4),
-                in_=raws[hg][:, :, :, 128 * jj + av : 128 * jj + 128].rearrange("p c t (b i) -> p c b t i", i=4),
+                out=gws[k][:, :, av:128, :].rearrange("p c (b i) t -> p c b t i", i=8),
+                in_=raws[hg][:, :, :, 128 * jj + av : 128 * jj + 128].rearrange("p c t (b i) -> p c b t i", i=8),
             )
 
         def quant(k):
@@ -249,9 +249,7 @@ def tile_yarnixcellv4_pa_kernel(
             nc.scalar.activation(
                 out=st[:, :, o : o + 128], in_=banks[k][:], func=ACT.Copy, scale=TWO_PI if gt == 0 else -1.0
             )
-            if k == 22:
-                nc.sync.dma_start(out=out0_v[:, :, 768:896], in_=st[:, :, 0:128])
-            elif j % 2 == 1:
+            if j % 2 == 1:
                 u0 = 128 * (j - 1)
                 nc.sync.dma_start(out=(out1_v if gt == 0 else out0_v)[:, :, u0 : u0 + 256], in_=st[:])
 
@@ -261,6 +259,14 @@ def tile_yarnixcellv4_pa_kernel(
             last[i] = mxp.tile([P, 512], F32, name="last%d" % i, tag="acc")
             for c in range(4):
                 multiply(last[i][:, 0:256], 23, c, 256 * i, 256)
+
+        def turn_part(bank, src, r0, first):
+            nb = bank[:].shape[1]
+            for b in range(nb):
+                nc.tensor.matmul(
+                    out=bank[:, b, :], lhsT=src[:, r0 + P * b : r0 + P * b + P], rhs=ident_f[:],
+                    is_transpose=True, start=(first and b == 0), stop=(not first and b == nb - 1),
+                )
 
         def last_v(i):
             rt = rts[7][:, 256 * i : 256 * i + 256]
@@ -277,24 +283,15 @@ def tile_yarnixcellv4_pa_kernel(
             zt = zts[7][:, 256 * i : 256 * i + 256]
             nc.vector.scalar_tensor_tensor(out=rt, in0=rt, scalar=-1.0, in1=zt, op0=ALU.mult, op1=ALU.mult)
 
-        def last_t(i):
-            bank = tpp.tile([P, 2, P], F32, name="plast", tag="tp")
-            for q in range(4):
-                src = wts[7] if q < 2 else rts[7]
-                b = 2 * i + q % 2
-                nc.tensor.matmul(
-                    out=bank[:, q % 2, :], lhsT=src[:, 128 * b : 128 * b + 128], rhs=ident_f[:],
-                    is_transpose=True, start=(q == 0), stop=(q == 3),
-                )
-            banks[("last", i)] = bank
-
         def last_leave(i):
-            st = stp.tile([P, 2, P], F32, name="stl%d" % i, tag="stl")
+            out = stages["end"][:, 2 * i : 2 * i + 2, 128:256]
             if i == 0:
-                nc.scalar.activation(out=st[:], in_=banks[("last", i)][:], func=ACT.Copy, scale=-1.0)
+                nc.scalar.activation(out=out, in_=banks[("last", i)][:], func=ACT.Copy, scale=-1.0)
             else:
-                nc.vector.tensor_scalar_mul(out=st[:], in0=banks[("last", i)][:], scalar1=-1.0)
-            nc.sync.dma_start(out=out0_v[:, 2 * i : 2 * i + 2, 896:1024], in_=st[:])
+                nc.vector.tensor_scalar_mul(out=out, in0=banks[("last", i)][:], scalar1=-1.0)
+            nc.sync.dma_start(
+                out=out0_v[:, 2 * i : 2 * i + 2, 768:1024], in_=stages["end"][:, 2 * i : 2 * i + 2, :]
+            )
 
         load_rows(x_sb, x, 2)
         load_piece(0, 0)
@@ -438,35 +435,27 @@ def tile_yarnixcellv4_pa_kernel(
                         regroup_s(k)
             last_mx(0)
             last_mx(1)
-            for k in range(20, 22):
-                if turn_step(k) > 22 and second_step(k) <= 22:
-                    second_t(k)
-            for k in range(20, 23):
-                if stt_step(k) > 22:
-                    gate_n_v(k)
+            second_t(20)
+            bank22 = tpp.tile([P, 4, P], F32, name="bank22", tag="tp")
             for i in range(2):
-                last_v(i)
-            for k in range(18, 22):
-                if second_step(k) > 22:
-                    second_v(k)
-            for k in range(18, 22):
-                if leave_step(k) > 22 and turn_step(k) <= 22:
-                    leave(k)
-            for k in range(20, 23):
-                if tanh_step(k) > 22:
-                    gate_n_s(k)
-            for i in range(2):
-                last_s(i)
-            for k in range(18, 22):
-                if second_step(k) > 22:
-                    second_t(k)
+                banks[("last", i)] = tpp.tile([P, 2, P], F32, name="end%d" % i, tag="tp")
+            gate_n_v(22)
+            last_v(0)
+            last_v(1)
+            second_v(21)
+            gate_n_s(22)
+            last_s(0)
+            last_s(1)
+            second_t(21)
             second_v(22)
-            second_t(22)
-            for k in range(18, 22):
-                if turn_step(k) > 22:
-                    leave(k)
-            leave(22)
+            turn_part(bank22, wts[6], 0, True)
+            turn_part(bank22, rts[6], 0, False)
+            leave(20)
+            leave(21)
+            stages["end"] = stp.tile([P, 4, 256], F32, name="ste", tag="st2")
+            nc.scalar.activation(out=stages["end"][:, :, 0:128], in_=bank22[:], func=ACT.Copy, scale=-1.0)
             for i in range(2):
                 last_v2(i)
-                last_t(i)
+                turn_part(banks[("last", i)], wts[7], 256 * i, True)
+                turn_part(banks[("last", i)], rts[7], 256 * i, False)
                 last_leave(i)

import math
from contextlib import ExitStack

import concourse.mybir as mybir
from concourse.masks import make_identity

FLOPS = 2 * 512 * 2048 * 3072

BF16 = mybir.dt.bfloat16
F32 = mybir.dt.float32
U32 = mybir.dt.uint32
U8 = mybir.dt.uint8
FP8X4 = mybir.dt.float8_e4m3fn_x4
ACT = mybir.ActivationFunctionType
ALU = mybir.AluOpType
PINNED = {mybir.EngineType.DVE, mybir.EngineType.Activation, mybir.EngineType.PE}

P = 128
TWO_PI = 2.0 * math.pi
GATE_COL = (1024, 0, 2048)
GATE_BIAS = (8, 0, 16)
AV_HEAD = (288, 320)
AV = {2: 72, 3: 64, 4: 72, 5: 72}


def tile_yarnixcellv4_pa_kernel(
    tc, x, h_state, local_angle, persistence, weight_ih, weight_hh, bias, out_0, out_1
):
    nc = tc.nc
    with ExitStack() as ctx:
        const = ctx.enter_context(tc.tile_pool(name="const", bufs=1))
        rawp = ctx.enter_context(tc.tile_pool(name="rawp", bufs=4))
        gwp = ctx.enter_context(tc.tile_pool(name="gwp", bufs=4))
        wcp = ctx.enter_context(tc.tile_pool(name="wcp", bufs=4))
        eap = ctx.enter_context(tc.tile_pool(name="eap", bufs=5))
        app = ctx.enter_context(tc.tile_pool(name="app", bufs=3))
        stp = ctx.enter_context(tc.tile_pool(name="stp", bufs=2))
        mxp = ctx.enter_context(tc.psum_pool(name="mxp", bufs=4))
        tpp = ctx.enter_context(tc.psum_pool(name="tpp", bufs=4))

        warm = const.tile([P, 1], F32, name="warm")
        nc.vector.memset(warm[:], 0.0)
        ident_b = const.tile([P, P], BF16, name="ident_b")
        ident_f = const.tile([P, P], F32, name="ident_f")
        make_identity(nc, ident_f[:])
        make_identity(nc, ident_b[:])
        bp = const.tile([P, P], BF16, name="bp")
        bcol = const.tile([P, 32], F32, name="bcol")
        persp = const.tile([P, 8], F32, name="persp")
        x_sb = const.tile([P, 4096], BF16, name="x_sb")
        h_sb = const.tile([P, 4096], BF16, name="h_sb")
        a_sb = const.tile([P, 4096], BF16, name="a_sb")
        gx = const.tile([P, 4096], BF16, name="gx", align_bytes=64)
        gh = const.tile([P, 4096], BF16, name="gh", align_bytes=64)
        xc = const.tile([P, 1024], U32, name="xc", align_bytes=64)
        xs = const.tile([P, 1024], U8, name="xs", align_bytes=64)
        hc = const.tile([P, 1024], U32, name="hc", align_bytes=64)
        hs = const.tile([P, 1024], U8, name="hs", align_bytes=64)
        wch = [const.tile([P, 4, 512], U32, name="wch%d" % hg, align_bytes=64) for hg in range(2)]
        wsh = [const.tile([P, 4, 512], U8, name="wsh%d" % hg, align_bytes=64) for hg in range(2)]

        nc.vector.memset(bp[:], 0.0)
        nc.scalar.dma_start(out=bp[0:24, :], in_=bias.rearrange("(r c) -> r c", c=P))
        nc.scalar.dma_start(out=bp[24:32, :], in_=persistence.rearrange("(r c) -> r c", c=P))

        raws = {}
        gws = {}
        wcs = {}
        wss = {}
        accs = {}
        zts = {}
        wts = {}
        rts = {}
        qts = {}
        ahs = {}
        banks = {}
        stages = {}

        def load_piece(hg, c):
            if c == 0:
                raws[hg] = rawp.tile([P, 4, 4, 512], BF16, name="raw%d" % hg, tag="raw")
            col = GATE_COL[hg % 3] + 512 * (hg // 3)
            src = weight_ih if c < 2 else weight_hh
            for u in range(2):
                r0 = 512 * (c % 2) + 256 * u
                nc.sync.dma_start(
                    out=raws[hg][:, c, 2 * u : 2 * u + 2, :],
                    in_=src[r0 : r0 + 256, col : col + 512].rearrange("(q e) w -> q e w", e=2),
                )

        def load_rows(t, src, pieces):
            tv = t[:].rearrange("p (b k) -> p b k", b=4)
            sv = src.rearrange("(p b) k -> p b k", b=4)
            n = 4 // pieces
            for k in range(pieces):
                nc.sync.dma_start(out=tv[:, n * k : n * k + n, :], in_=sv[:, n * k : n * k + n, :])

        def copy_on(on_scalar, out, in_):
            if on_scalar:
                nc.scalar.copy(out=out, in_=in_)
            else:
                nc.vector.tensor_copy(out=out, in_=in_)

        def head_regroup(hg, c):
            gw = gwp.tile([P, 512, 4], BF16, name="gwh%d_%d" % (hg, c), tag="gw", align_bytes=64)
            nc.vector.tensor_copy(
                out=gw[:, 0 : AV_HEAD[hg], :].rearrange("p (b i) t -> p b t i", i=8),
                in_=raws[hg][:, c, :, 0 : AV_HEAD[hg]].rearrange("p t (b i) -> p b t i", i=8),
            )
            nc.scalar.copy(
                out=gw[:, AV_HEAD[hg] : 512, :].rearrange("p (b i) t -> p b t i", i=8),
                in_=raws[hg][:, c, :, AV_HEAD[hg] : 512].rearrange("p t (b i) -> p b t i", i=8),
            )
            gws[("h", hg, c)] = gw

        def head_quant(hg, c):
            nc.vector.quantize_mx(
                out=wch[hg][:, c, :].bitcast(FP8X4),
                scales=wsh[hg][:, c, :],
                in_=gws[("h", hg, c)][:].rearrange("p w t -> p (w t)"),
            )

        def regroup_v(k):
            hg, jj = divmod(k, 4)
            av = AV[hg]
            gws[k] = gwp.tile([P, 4, 128, 4], BF16, name="gw%d" % k, tag="gw", align_bytes=64)
            nc.vector.tensor_copy(
                out=gws[k][:, :, 0:av, :].rearrange("p c (b i) t -> p c b t i", i=8),
                in_=raws[hg][:, :, :, 128 * jj : 128 * jj + av].rearrange("p c t (b i) -> p c b t i", i=8),
            )

        def regroup_s(k):
            hg, jj = divmod(k, 4)
            av = AV[hg]
            nc.scalar.copy(
                out=gws[k][:, :, av:128, :].rearrange("p c (b i) t -> p c b t i", i=8),
                in_=raws[hg][:, :, :, 128 * jj + av : 128 * jj + 128].rearrange("p c t (b i) -> p c b t i", i=8),
            )

        def quant(k):
            wcs[k] = wcp.tile([P, 4, 128], U32, name="wc%d" % k, tag="wc", align_bytes=64)
            wss[k] = wcp.tile([P, 4, 128], U8, name="ws%d" % k, tag="ws", align_bytes=64)
            nc.vector.quantize_mx(
                out=wcs[k][:].rearrange("p c w -> p (c w)").bitcast(FP8X4),
                scales=wss[k][:].rearrange("p c w -> p (c w)"),
                in_=gws[k][:].rearrange("p c w t -> p (c w t)"),
            )

        def mx_pass(k, c):
            if c == 0:
                accs[k] = mxp.tile([P, 512], F32, name="acc%d" % k, tag="acc")
            multiply(accs[k][:], k, c, 0, 512)

        def multiply(out, k, c, r0, rn):
            if k < 8:
                hg, jj = divmod(k, 4)
                lw, ls = wch[hg][:, c, 128 * jj : 128 * jj + 128], wsh[hg][:, c, 128 * jj : 128 * jj + 128]
            else:
                lw, ls = wcs[k][:, c, :], wss[k][:, c, :]
            rc, rs = (xc, xs) if c < 2 else (hc, hs)
            r = 512 * (c % 2) + r0
            nc.tensor.matmul_mx(
                out=out,
                lhsT=lw.bitcast(FP8X4),
                lhsT_scale=ls,
                rhs=rc[:, r : r + rn].bitcast(FP8X4),
                rhs_scale=rs[:, r : r + rn],
                start=(c == 0),
                stop=(c == 3),
            )

        def bias_col(gt, j):
            k = GATE_BIAS[gt] + j
            return bcol[:, k : k + 1]

        def kind(k):
            hg, jj = divmod(k, 4)
            return hg % 3, 4 * (hg // 3) + jj

        def gate_sigmoid(k):
            gt, j = kind(k)
            dst = zts if gt == 0 else rts
            dst[j] = eap.tile([P, 512], F32, name="g%d" % k, tag="z" if gt == 0 else "r")
            nc.scalar.activation(out=dst[j][:], in_=accs[k][:], func=ACT.Sigmoid, bias=bias_col(gt, j), scale=1.0)

        def gate_n_v(k):
            gt, j = kind(k)
            nc.vector.scalar_tensor_tensor(
                out=rts[j][:], in0=accs[k][:], scalar=bias_col(2, j), in1=rts[j][:], op0=ALU.add, op1=ALU.mult
            )

        def gate_n_s(k):
            gt, j = kind(k)
            nc.scalar.activation(out=rts[j][:], in_=rts[j][:], func=ACT.Tanh)

        def transpose_ah(j):
            ah = tpp.tile([P, 2, 512], BF16, name="ah", tag="tp")
            for s, src in enumerate((a_sb, h_sb)):
                for b in range(4):
                    k0 = b * 1024 + 128 * j
                    nc.tensor.transpose(ah[:, s, 128 * b : 128 * b + 128], src[:, k0 : k0 + 128], ident_b[:])
            ahs[j] = ah

        def second_v(k):
            gt, j = kind(k)
            if gt == 0:
                wts[j] = eap.tile([P, 512], F32, name="w%d" % k, tag="w")
                qts[j] = app.tile([P, 512], F32, name="q%d" % k, tag="q")
                nc.vector.scalar_tensor_tensor(
                    out=qts[j][:], in0=ahs[j][:, 0, :], scalar=persp[:, j : j + 1], in1=zts[j][:], op0=ALU.mult, op1=ALU.add
                )
                nc.vector.scalar_tensor_tensor(
                    out=wts[j][:], in0=zts[j][:], scalar=1.0, in1=ahs[j][:, 1, :], op0=ALU.subtract, op1=ALU.mult
                )
            elif gt == 2:
                nc.vector.scalar_tensor_tensor(
                    out=rts[j][:], in0=rts[j][:], scalar=-1.0, in1=zts[j][:], op0=ALU.mult, op1=ALU.mult
                )

        def second_t(k):
            gt, j = kind(k)
            if gt == 0:
                bank = tpp.tile([P, 4, P], F32, name="pra", tag="tp")
                for b in range(4):
                    nc.tensor.transpose(bank[:, b, :], qts[j][:, 128 * b : 128 * b + 128], ident_f[:])
                banks[k] = bank
            elif gt == 2:
                bank = tpp.tile([P, 4, P], F32, name="phb", tag="tp")
                for i in range(8):
                    src = wts[j] if i < 4 else rts[j]
                    b = i % 4
                    nc.tensor.matmul(
                        out=bank[:, b, :], lhsT=src[:, 128 * b : 128 * b + 128], rhs=ident_f[:],
                        is_transpose=True, start=(i == 0), stop=(i == 7),
                    )
                banks[k] = bank

        out0_v = out_0.rearrange("(p b) u -> p b u", b=4)
        out1_v = out_1.rearrange("(p b) u -> p b u", b=4)

        def leave(k):
            gt, j = kind(k)
            if gt == 1:
                return
            if j % 2 == 0:
                stages[gt] = stp.tile([P, 4, 256], F32, name="st%d" % gt, tag="st%d" % gt)
            st = stages[gt]
            o = 128 * (j % 2)
            nc.scalar.activation(
                out=st[:, :, o : o + 128], in_=banks[k][:], func=ACT.Copy, scale=TWO_PI if gt == 0 else -1.0
            )
            if j % 2 == 1:
                u0 = 128 * (j - 1)
                nc.sync.dma_start(out=(out1_v if gt == 0 else out0_v)[:, :, u0 : u0 + 256], in_=st[:])

        last = {}

        def last_mx(i):
            last[i] = mxp.tile([P, 512], F32, name="last%d" % i, tag="acc")
            for c in range(4):
                multiply(last[i][:, 0:256], 23, c, 256 * i, 256)

        def turn_part(bank, src, r0, first):
            nb = bank[:].shape[1]
            for b in range(nb):
                nc.tensor.matmul(
                    out=bank[:, b, :], lhsT=src[:, r0 + P * b : r0 + P * b + P], rhs=ident_f[:],
                    is_transpose=True, start=(first and b == 0), stop=(not first and b == nb - 1),
                )

        def last_v(i):
            rt = rts[7][:, 256 * i : 256 * i + 256]
            nc.vector.scalar_tensor_tensor(
                out=rt, in0=last[i][:, 0:256], scalar=bias_col(2, 7), in1=rt, op0=ALU.add, op1=ALU.mult
            )

        def last_s(i):
            rt = rts[7][:, 256 * i : 256 * i + 256]
            nc.scalar.activation(out=rt, in_=rt, func=ACT.Tanh)

        def last_v2(i):
            rt = rts[7][:, 256 * i : 256 * i + 256]
            zt = zts[7][:, 256 * i : 256 * i + 256]
            nc.vector.scalar_tensor_tensor(out=rt, in0=rt, scalar=-1.0, in1=zt, op0=ALU.mult, op1=ALU.mult)

        def last_leave(i):
            out = stages["end"][:, 2 * i : 2 * i + 2, 128:256]
            if i == 0:
                nc.scalar.activation(out=out, in_=banks[("last", i)][:], func=ACT.Copy, scale=-1.0)
            else:
                nc.vector.tensor_scalar_mul(out=out, in0=banks[("last", i)][:], scalar1=-1.0)
            nc.sync.dma_start(
                out=out0_v[:, 2 * i : 2 * i + 2, 768:1024], in_=stages["end"][:, 2 * i : 2 * i + 2, :]
            )

        load_rows(x_sb, x, 2)
        load_piece(0, 0)
        load_piece(0, 1)
        load_rows(h_sb, h_state, 2)
        load_piece(0, 2)
        load_piece(0, 3)
        load_piece(1, 0)
        load_piece(1, 1)
        load_piece(1, 2)
        av4 = a_sb[:].rearrange("p (b k) -> p b k", b=4)
        as4 = local_angle.rearrange("(p b) k -> p b k", b=4)
        nc.sync.dma_start(out=av4[:, :, 0:512], in_=as4[:, :, 0:512])
        load_piece(1, 3)
        for c in range(4):
            load_piece(2, c)
        nc.sync.dma_start(out=av4[:, :, 512:1024], in_=as4[:, :, 512:1024])
        for hg in range(3, 6):
            for c in range(4):
                load_piece(hg, c)

        def word_transpose(src, hf, g):
            xt = tpp.tile([P, 2, 256], F32, name="xt", tag="tp")
            sw = src[:].bitcast(F32)
            for u in range(2):
                for b2 in range(2):
                    w0 = (2 * hf + b2) * 512 + 256 * g + 128 * u
                    nc.tensor.transpose(xt[:, u, 128 * b2 : 128 * b2 + 128], sw[:, w0 : w0 + 128], ident_f[:])
            return xt

        def word_leave(dst, hf, g, xt, on_scalar):
            o0 = g * 1024 + hf * 512
            copy_on(
                on_scalar,
                dst[:].bitcast(F32)[:, o0 : o0 + 512].rearrange("p (r u) -> p r u", u=2),
                xt[:].rearrange("p u r -> p r u"),
            )

        def sig_step(k):
            return k + 1

        def stt_step(k):
            return k + 1

        def tanh_step(k):
            return k + 1

        def second_step(k):
            if k < 4:
                return k + 4
            return k + (2 if kind(k)[0] == 0 else 2)

        def turn_step(k):
            return second_step(k) + 1

        def leave_step(k):
            return turn_step(k) + 1

        def r_step(k):
            return k - 4

        def q_step(k):
            return r_step(k) + 2

        with tc.manual_schedule(engines=PINNED):
            nc.scalar.activation(out=warm[:], in_=warm[:], func=ACT.Sigmoid)
            for hf in range(2):
                for g in range(2):
                    xt = word_transpose(x_sb, hf, g)
                    word_leave(gx, hf, g, xt, g == 1)
            head_regroup(0, 0)
            nc.vector.quantize_mx(out=xc[:].bitcast(FP8X4), scales=xs[:], in_=gx[:])
            pb = tpp.tile([P, P], BF16, name="pb", tag="tp")
            nc.tensor.transpose(pb[:], bp[:], ident_b[:])
            head_regroup(0, 1)
            head_quant(0, 0)
            nc.vector.tensor_copy(out=bcol[:], in_=pb[:, 0:32])
            head_quant(0, 1)
            nc.vector.tensor_scalar_mul(out=persp[:], in0=bcol[:, 24:32], scalar1=1.0 / TWO_PI)
            for hf in range(2):
                for g in range(2):
                    xt = word_transpose(h_sb, hf, g)
                    word_leave(gh, hf, g, xt, True)
            for c in range(2):
                for k in range(4):
                    mx_pass(k, c)
            head_regroup(0, 2)
            nc.vector.quantize_mx(out=hc[:].bitcast(FP8X4), scales=hs[:], in_=gh[:])
            head_regroup(0, 3)
            head_quant(0, 2)
            for k in range(4):
                mx_pass(k, 2)
            head_regroup(1, 0)
            head_quant(0, 3)
            for k in range(4):
                mx_pass(k, 3)
            head_regroup(1, 1)
            head_quant(1, 0)
            gate_sigmoid(0)
            head_regroup(1, 2)
            head_quant(1, 1)
            gate_sigmoid(1)
            transpose_ah(0)
            transpose_ah(1)
            head_regroup(1, 3)
            head_quant(1, 2)
            gate_sigmoid(2)
            head_quant(1, 3)

            for s in range(4, 23):
                for c in range(4):
                    mx_pass(s, c)
                for k in range(2, 22):
                    if second_step(k) == s + 1 and kind(k)[0] == 0:
                        transpose_ah(kind(k)[1])
                for k in range(22):
                    if turn_step(k) == s:
                        second_t(k)
                for k in range(4, 22):
                    if stt_step(k) == s and kind(k)[0] == 2:
                        gate_n_v(k)
                for k in range(22):
                    if second_step(k) == s:
                        second_v(k)
                for k in range(8, 24):
                    if q_step(k) == s:
                        quant(k)
                for k in range(8, 24):
                    if r_step(k) == s:
                        regroup_v(k)
                for k in range(22):
                    if leave_step(k) == s:
                        leave(k)
                for k in range(3, 22):
                    if sig_step(k) == s and kind(k)[0] != 2:
                        gate_sigmoid(k)
                    if tanh_step(k) == s and kind(k)[0] == 2:
                        gate_n_s(k)
                for k in range(8, 24):
                    if r_step(k) == s:
                        regroup_s(k)
            last_mx(0)
            last_mx(1)
            second_t(20)
            bank22 = tpp.tile([P, 4, P], F32, name="bank22", tag="tp")
            for i in range(2):
                banks[("last", i)] = tpp.tile([P, 2, P], F32, name="end%d" % i, tag="tp")
            gate_n_v(22)
            last_v(0)
            last_v(1)
            second_v(21)
            gate_n_s(22)
            last_s(0)
            last_s(1)
            second_t(21)
            second_v(22)
            turn_part(bank22, wts[6], 0, True)
            turn_part(bank22, rts[6], 0, False)
            leave(20)
            leave(21)
            stages["end"] = stp.tile([P, 4, 256], F32, name="ste", tag="st2")
            nc.scalar.activation(out=stages["end"][:, :, 0:128], in_=bank22[:], func=ACT.Copy, scale=-1.0)
            for i in range(2):
                last_v2(i)
                turn_part(banks[("last", i)], wts[7], 256 * i, True)
                turn_part(banks[("last", i)], rts[7], 256 * i, False)
                last_leave(i)
